import numpy as np
import ml_dtypes


def mxq(x, axis, fmt="e4m3"):
    dtype, down = {"e4m3": (ml_dtypes.float8_e4m3fn, 7), "e5m2": (ml_dtypes.float8_e5m2, 14)}[fmt]
    v = np.moveaxis(np.asarray(x, np.float32).astype(ml_dtypes.bfloat16).astype(np.float64), axis, -1)
    blocks = v.reshape(v.shape[:-1] + (-1, 32))
    amax = np.abs(blocks).max(-1, keepdims=True)
    byte = np.maximum(np.where(amax > 0, np.frexp(amax)[1] - 1 + 127, 0) - down, 1)
    scale = np.exp2(byte - 127.0)
    codes = (blocks / scale).astype(np.float32).astype(dtype).astype(np.float64)
    return np.moveaxis((codes * scale).reshape(v.shape), -1, axis)


WIDE = False


def mx_kscale(k):
    if not WIDE:
        return np.ones(k)
    levels = np.array([10, -10, 5, -5, 0])
    a = np.random.permutation(np.resize(levels, k // 512 * 4)).reshape(k // 512, 4)
    idx = np.arange(k)
    return np.exp2(a[idx // 512, idx % 128 // 32])


BF16 = ml_dtypes.bfloat16


def bf(x):
    return np.asarray(x, np.float32).astype(BF16)


def f64(x):
    return np.asarray(x).astype(np.float64)


E2M1 = np.array([0.0, 0.5, 1.0, 1.5, 2.0, 3.0, 4.0, 6.0, -0.0, -0.5, -1.0, -1.5, -2.0, -3.0, -4.0, -6.0])


def pack_weight(w, fmt):
    k, n = w.shape
    w = f64(bf(w)).reshape(k // 32, 32, n)
    amax = np.abs(w).max(1)
    if fmt == "e4m3":
        byte = np.frexp(amax)[1] - 1 + 127 - 7
    else:
        mant, ex = np.frexp(amax / 6.0)
        byte = np.where(mant > 0.5, ex, ex - 1) + 127
    byte = np.clip(np.where(amax > 0, byte, 1), 1, 254)
    scaled = (w * np.exp2(127.0 - byte)[:, None, :]).reshape(k, n).astype(np.float32)
    by_word = np.ascontiguousarray(scaled.reshape(k // 512, 128, 4, n).transpose(0, 1, 3, 2))
    if fmt == "e4m3":
        words = by_word.astype(ml_dtypes.float8_e4m3fn).view(np.uint8)
    else:
        c = by_word.astype(ml_dtypes.float4_e2m1fn).view(np.uint8) & 0xF
        words = c[..., 0::2] | (c[..., 1::2] << 4)
    return np.ascontiguousarray(words), np.ascontiguousarray(byte.astype(np.uint8).reshape(k // 512, 16, n))


def unpack_weight(words, scales, fmt):
    g, p, n, _ = words.shape
    if fmt == "e4m3":
        vals = np.ascontiguousarray(words).view(ml_dtypes.float8_e4m3fn).astype(np.float64)
    else:
        nib = np.empty((g, p, n, 4), np.uint8)
        nib[..., 0::2] = words & 0xF
        nib[..., 1::2] = words >> 4
        vals = E2M1[nib]
    vals = vals * np.repeat(np.exp2(scales.astype(np.float64) - 127.0), 8, axis=1)[..., None]
    return vals.transpose(0, 1, 3, 2).reshape(g * 512, n)

def pack4(w):
    words, scales = pack_weight(w, "e2m1")
    return words.reshape(words.shape[0], 128, -1), scales


def unpack4(words, scales):
    return unpack_weight(words.reshape(words.shape[0], 128, -1, 2), scales, "e2m1")


B, C, T, H = 4, 256, 2048, 1024
EPS_LN = 1e-5
EPS_STD = 1e-5


def ln_dim1(z, g, b):
    mu = z.mean(axis=1, keepdims=True)
    var = ((z - mu) ** 2).mean(axis=1, keepdims=True)
    return (z - mu) / np.sqrt(var + EPS_LN) * g[None, :, None] + b[None, :, None]


def stats(x, m):
    mean = (m * x).sum(axis=2)
    std = np.sqrt(np.maximum((m * x * x).sum(axis=2) - mean ** 2, EPS_STD))
    return mean, std


def setup_inputs():
    s = mx_kscale(H)
    drop = np.random.randint(B, size=T)
    mask = (np.arange(B)[:, None, None] != drop[None, None, :]) * 1.0
    off = 0.5 * np.random.standard_normal((B, C, 1))
    gain = 0.5 + np.random.random((B, C, 1))
    pad = np.random.standard_normal((B, C, 1)) * (1.0 - mask)
    x = off + gain * np.random.standard_normal((B, C, T)) + pad
    h = bf(np.tanh(np.random.standard_normal((B, H, T))) * s[None, :, None])
    w2 = np.random.standard_normal((C, H)) * 3.0 / np.sqrt(H) / s[None, :]
    w2_words, w2_scales = pack4(np.ascontiguousarray(w2.T))
    return {"h": h,
            "x": bf(x),
            "mask": bf(mask),
            "w2_words": w2_words,
            "w2_scales": w2_scales,
            "b2": bf(0.1 * np.random.standard_normal(C)),
            "g2": bf(1.0 + 0.1 * np.random.standard_normal(2 * C)),
            "be2": bf(0.1 * np.random.standard_normal(2 * C))}


def reference(h, x, mask, w2_words, w2_scales, b2, g2, be2):
    x, mask = f64(x), f64(mask)
    alpha = (unpack4(w2_words, w2_scales).T @ mxq(f64(h), 1, "e4m3")) + f64(b2)[None, :, None]
    alpha = np.where(mask == 0, -np.inf, alpha)
    e = np.exp(alpha - alpha.max(axis=2, keepdims=True))
    alpha = e / e.sum(axis=2, keepdims=True)
    mean, std = stats(x, alpha)
    out = np.concatenate([mean, std], axis=1)[:, :, None]
    return ln_dim1(out, f64(g2), f64(be2))

@@ -1,0 +1,386 @@
+import concourse.bass as bass
+import concourse.mybir as mybir
+import concourse.tile as tile
+from concourse.masks import make_identity
+
+FLOPS = 2 * 4 * 256 * 1024 * 2048
+
+F32 = mybir.dt.float32
+BF16 = mybir.dt.bfloat16
+I32 = mybir.dt.int32
+U32 = mybir.dt.uint32
+U8 = mybir.dt.uint8
+FP8X4 = mybir.dt.float8_e4m3fn_x4
+FP4X4 = mybir.dt.float4_e2m1fn_x4
+ALU = mybir.AluOpType
+ACT = mybir.ActivationFunctionType
+AX = mybir.AxisListType
+
+P = 128
+PACK = 4
+K_PASS = P * PACK
+B, C, T, H = 4, 256, 2048, 1024
+PASSES = H // K_PASS
+HALVES = C // P
+FRAMES = 512
+CHUNKS = T // FRAMES
+TILES = FRAMES // P
+UTT_TILES = T // P
+EPS_LN = 1e-5
+EPS_STD = 1e-5
+MASKED = 1.0e30
+
+SLOTS = B * CHUNKS
+LOAD_AHEAD = 3
+EXP_LAG = 4
+PRODUCT_LAG = 6
+STEPS = SLOTS + PRODUCT_LAG
+EARLY_SLOTS = 7
+EARLY_FRAMES = 384
+LATE_FRAMES = 256
+GPSIMD_FRAMES = 128
+BRIDGE_FRAMES = 208
+HEAD_FRAMES = 320
+
+
+def tile_attentivestatspool_pb_t_kernel(
+    tc, h, x, mask, w2_words, w2_scales, b2, g2, be2, out
+):
+    nc = tc.nc
+    with tc.tile_pool(name="const", bufs=1) as const, tc.tile_pool(
+        name="raw", bufs=8
+    ) as raw_pool, tc.tile_pool(name="grouped", bufs=2) as grouped_pool, tc.tile_pool(
+        name="quant", bufs=3
+    ) as quant, tc.tile_pool(name="turned", bufs=2) as turned_pool, tc.tile_pool(
+        name="feat", bufs=3
+    ) as feat, tc.tile_pool(name="score", bufs=4) as score, tc.tile_pool(
+        name="prod", bufs=2
+    ) as prod, tc.psum_pool(name="acc", bufs=4) as acc_pool, tc.psum_pool(
+        name="back", bufs=4
+    ) as back_pool, tc.manual_schedule():
+        ident = const.tile([P, P], F32)
+        make_identity(nc, ident[:])
+        ident_bf = const.tile([P, P], BF16)
+        make_identity(nc, ident_bf[:])
+        v = const.tile([P, 2 * HALVES, P], F32)
+        nc.gpsimd.memset(v[:], 0.0)
+        sum_e4 = const.tile([P, HALVES, B, CHUNKS], F32)
+        sum_ex = const.tile([P, HALVES, B], F32)
+        sum_exx = const.tile([P, HALVES, B], F32)
+        neg_max4 = const.tile([P, B, HALVES, CHUNKS], F32)
+        neg_max = const.tile([P, B, HALVES], F32)
+
+        raw = {}
+        grouped = {}
+        codes = {}
+        planes = {}
+        acc = {}
+        turned = {}
+        first = {}
+        again = {}
+        x_sb = {}
+        e = {}
+        ex = {}
+
+        def load(s):
+            b, c = divmod(s, CHUNKS)
+            h_rows = h[b].rearrange("(g p j) n -> g p j n", p=P, j=PACK)
+            for g in range(PASSES):
+                raw[s, g] = raw_pool.tile([P, PACK, FRAMES], BF16, name="raw")
+                nc.sync.dma_start(
+                    out=raw[s, g][:], in_=h_rows[g, :, :, c * FRAMES : (c + 1) * FRAMES]
+                )
+
+        def load_x(b):
+            x_sb[b] = feat.tile([P, HALVES, T], BF16, name="x_sb")
+            nc.sync.dma_start(out=x_sb[b][:], in_=x[b].rearrange("(hf p) n -> p hf n", p=P))
+
+        def views(s, g):
+            dst = grouped[s][:, g].rearrange("p (c i) j -> p c j i", i=4)
+            src = raw[s, g][:].rearrange("p j (c i) -> p c j i", i=4)
+            return dst, src
+
+        def regroup_start(s):
+            grouped[s] = grouped_pool.tile(
+                [P, PASSES, FRAMES, PACK], BF16, name="grouped", align_bytes=64
+            )
+            if s >= 2:
+                f = FRAMES - GPSIMD_FRAMES
+                nc.gpsimd.tensor_scalar(
+                    out=grouped[s][:, 1, f:, :],
+                    in0=raw[s, 1][:, :, f:].rearrange("p j n -> p n j"),
+                    scalar1=1.0,
+                    scalar2=0.0,
+                    op0=ALU.mult,
+                    op1=ALU.add,
+                )
+
+        def bridge(s):
+            return EXP_LAG < s < EARLY_SLOTS
+
+        def regroup_first_pass(s):
+            dst, src = views(s, 0)
+            cut = (BRIDGE_FRAMES if bridge(s) else 0) // 4
+            nc.scalar.copy(out=dst[:, cut:], in_=src[:, cut:])
+
+        def regroup_second_pass(s):
+            dst, src = views(s, 1)
+            end = (FRAMES - (GPSIMD_FRAMES if s >= 2 else 0)) // 4
+            cut = (EARLY_FRAMES if s < EARLY_SLOTS else LATE_FRAMES) // 4
+            nc.vector.tensor_copy(out=dst[:, 0:cut], in_=src[:, 0:cut])
+            if bridge(s):
+                dst0, src0 = views(s, 0)
+                nc.vector.tensor_copy(
+                    out=dst0[:, 0 : BRIDGE_FRAMES // 4], in_=src0[:, 0 : BRIDGE_FRAMES // 4]
+                )
+            if cut < end:
+                nc.scalar.copy(out=dst[:, cut:end], in_=src[:, cut:end])
+
+        def quantise(s):
+            codes[s] = quant.tile([P, PASSES * FRAMES], U32, name="codes", align_bytes=64)
+            planes[s] = quant.tile([P, PASSES * FRAMES], U8, name="planes", align_bytes=64)
+            nc.vector.quantize_mx(
+                out=codes[s][:].bitcast(FP8X4),
+                scales=planes[s][:],
+                in_=grouped[s][:].rearrange("p g n j -> p (g n j)"),
+            )
+
+        def multiply(s):
+            for k in range(TILES // 2):
+                acc[s, k] = acc_pool.tile([P, 2 * C], F32, name="acc")
+            for i in range(TILES):
+                for hf in range(HALVES):
+                    for g in range(PASSES):
+                        cols = slice(g * FRAMES + i * P, g * FRAMES + (i + 1) * P)
+                        at = (i % 2) * C + hf * P
+                        nc.tensor.matmul_mx(
+                            out=acc[s, i // 2][:, at : at + P],
+                            lhsT=codes[s][:, cols].bitcast(FP8X4),
+                            lhsT_scale=planes[s][:, cols],
+                            rhs=w_words[:, g, 2 * P * hf : 2 * P * (hf + 1)].bitcast(FP4X4),
+                            rhs_scale=w_planes[:, g, P * hf : P * (hf + 1)],
+                            start=(g == 0),
+                            stop=(g == PASSES - 1),
+                        )
+
+        def empty(s):
+            b, c = divmod(s, CHUNKS)
+            if c == 0:
+                turned[b] = turned_pool.tile([P, UTT_TILES, C], F32, name="turned")
+            for i in range(TILES):
+                n = c * TILES + i
+                nc.scalar.activation(
+                    out=turned[b][:, n, :],
+                    in_=acc[s, i // 2][:, (i % 2) * C : (i % 2 + 1) * C],
+                    func=ACT.Identity,
+                    bias=penalty[:, b * UTT_TILES + n : b * UTT_TILES + n + 1],
+                    scale=1.0,
+                )
+
+        def turn(b, c, hf):
+            bank = back_pool.tile([P, FRAMES], F32, name="back")
+            for i in range(TILES):
+                nc.tensor.transpose(
+                    out=bank[:, i * P : (i + 1) * P],
+                    in_=turned[b][:, c * TILES + i, hf * P : (hf + 1) * P],
+                    identity=ident[:],
+                )
+            return bank
+
+        def chunk_max(s):
+            b, c = divmod(s, CHUNKS)
+            for hf in range(HALVES):
+                nc.vector.tensor_reduce(
+                    out=neg_max4[:, b, hf, c : c + 1],
+                    in_=first[s, hf][:],
+                    axis=AX.X,
+                    op=ALU.max,
+                    negate=True,
+                )
+            if c == CHUNKS - 1:
+                nc.vector.tensor_reduce(
+                    out=neg_max[:, b, :], in_=neg_max4[:, b], axis=AX.X, op=ALU.min
+                )
+
+        def units(step):
+            found = []
+            for b in range(B):
+                k = 2 * (step - CHUNKS * b - EXP_LAG)
+                if 0 <= k < HALVES * CHUNKS:
+                    found.extend([(b, n % CHUNKS, n // CHUNKS) for n in (k, k + 1)])
+            return found
+
+        def exponent(b, c, hf):
+            if c == 0:
+                e[b, hf] = score.tile([P, T], F32, name="e")
+            nc.scalar.activation(
+                out=e[b, hf][:, c * FRAMES : (c + 1) * FRAMES],
+                in_=again[b, c, hf][:],
+                func=ACT.Exp,
+                bias=neg_max[:, b, hf : hf + 1],
+                scale=1.0,
+                accum_out=sum_e4[:, hf, b, c : c + 1],
+            )
+
+        def product(step):
+            n = step - PRODUCT_LAG
+            if n < 0 or n >= 2 * HALVES * B:
+                return
+            b, k = divmod(n, 2 * HALVES)
+            hf, second = divmod(k, 2)
+            if not second:
+                ex[b, hf] = prod.tile([P, T], F32, name="ex")
+                nc.vector.scalar_tensor_tensor(
+                    out=ex[b, hf][:],
+                    in0=e[b, hf][:],
+                    scalar=1.0,
+                    in1=x_sb[b][:, hf, :],
+                    op0=ALU.mult,
+                    op1=ALU.mult,
+                    accum_out=sum_ex[:, hf, b : b + 1],
+                )
+            else:
+                exx = prod.tile([P, T], F32, name="exx")
+                nc.vector.scalar_tensor_tensor(
+                    out=exx[:],
+                    in0=ex[b, hf][:],
+                    scalar=1.0,
+                    in1=x_sb[b][:, hf, :],
+                    op0=ALU.mult,
+                    op1=ALU.mult,
+                    accum_out=sum_exx[:, hf, b : b + 1],
+                )
+
+        load(0)
+        load(1)
+        mask_rows = const.tile([P, P], BF16)
+        nc.vector.memset(mask_rows[B * UTT_TILES : P, :], 0.0)
+        nc.sync.dma_start(
+            out=mask_rows[0 : B * UTT_TILES, :],
+            in_=mask.rearrange("b o (i p) -> (b o i) p", p=P),
+        )
+        w_words = const.tile([P, PASSES, 2 * C], U8, align_bytes=64)
+        nc.sync.dma_start(
+            out=w_words[:].bitcast(I32),
+            in_=w2_words.bitcast(I32).rearrange("g p n -> p g n"),
+        )
+        w_planes = const.tile([P, PASSES, C], U8, align_bytes=64)
+        nc.vector.memset(w_planes[:].rearrange("p g n -> p (g n)").bitcast(I32), 0)
+        for q in range(4):
+            nc.sync.dma_start(
+                out=w_planes[32 * q : 32 * q + 4].bitcast(I32),
+                in_=w2_scales.bitcast(I32)[:, 4 * q : 4 * q + 4, :].rearrange(
+                    "g r n -> r g n"
+                ),
+            )
+        for s in range(2, LOAD_AHEAD):
+            load(s)
+        mask_cols = back_pool.tile([P, P], BF16, name="back")
+        nc.tensor.transpose(out=mask_cols[:], in_=mask_rows[:], identity=ident_bf[:])
+        penalty = const.tile([P, B * UTT_TILES], F32)
+        regroup_start(0)
+        for g in range(PASSES):
+            dst, src = views(0, g)
+            nc.vector.tensor_copy(
+                out=dst[:, 0 : HEAD_FRAMES // 4], in_=src[:, 0 : HEAD_FRAMES // 4]
+            )
+            nc.scalar.copy(out=dst[:, HEAD_FRAMES // 4 :], in_=src[:, HEAD_FRAMES // 4 :])
+        regroup_start(1)
+
+        warm = const.tile([P, 1], F32)
+        inv_e = const.tile([P, HALVES, B], F32)
+        mean_sq = const.tile([P, HALVES, B], F32)
+        gain = const.tile([B, 2 * C], BF16)
+        offset = const.tile([B, 2 * C], BF16)
+        stats = const.tile([B, 2, 6], F32)
+        for step in range(STEPS):
+            if step + LOAD_AHEAD < SLOTS:
+                load(step + LOAD_AHEAD)
+            if step < SLOTS and step % CHUNKS == CHUNKS - 1:
+                load_x(step // CHUNKS)
+            if step == SLOTS - 1:
+                nc.sync.dma_start(out=gain[:], in_=g2.partition_broadcast(B))
+                nc.sync.dma_start(out=offset[:], in_=be2.partition_broadcast(B))
+            now = units(step)
+            if step < SLOTS:
+                quantise(step)
+                multiply(step)
+            for b, c, hf in now:
+                again[b, c, hf] = turn(b, c, hf)
+            if step == 0:
+                nc.vector.tensor_scalar(
+                    out=penalty[:],
+                    in0=mask_cols[:, 0 : B * UTT_TILES],
+                    scalar1=MASKED,
+                    scalar2=-MASKED,
+                    op0=ALU.mult,
+                    op1=ALU.add,
+                )
+            if step + 2 < SLOTS:
+                regroup_start(step + 2)
+            if 1 <= step <= SLOTS:
+                chunk_max(step - 1)
+            if step + 1 < SLOTS:
+                regroup_first_pass(step + 1)
+                regroup_second_pass(step + 1)
+            if step < SLOTS:
+                empty(step)
+                for hf in range(HALVES):
+                    first[step, hf] = turn(step // CHUNKS, step % CHUNKS, hf)
+            for b, c, hf in now:
+                exponent(b, c, hf)
+            if step == CHUNKS * (B - 1) + EXP_LAG + CHUNKS - 1:
+                nc.scalar.sqrt(out=warm[:], in_=ident[:, 0:1])
+            if step == STEPS - 1:
+                pooled = back_pool.tile([P, 2 * C], F32, name="back")
+                sum_e = const.tile([P, HALVES, B], F32)
+                nc.vector.tensor_reduce(out=sum_e[:], in_=sum_e4[:], axis=AX.X, op=ALU.add)
+                nc.vector.reciprocal(out=inv_e[:], in_=sum_e[:])
+                nc.vector.tensor_mul(out=v[:, 0:HALVES, 0:B], in0=sum_ex[:], in1=inv_e[:])
+                nc.vector.tensor_mul(
+                    out=mean_sq[:], in0=v[:, 0:HALVES, 0:B], in1=v[:, 0:HALVES, 0:B]
+                )
+                for q in range(HALVES):
+                    nc.tensor.transpose(
+                        out=pooled[:, q * P : (q + 1) * P], in_=v[:, q, :], identity=ident[:]
+                    )
+            product(step)
+
+        spread = const.tile([P, HALVES, B], F32)
+        nc.vector.tensor_mul(out=spread[:], in0=sum_exx[:], in1=inv_e[:])
+        nc.vector.tensor_sub(out=spread[:], in0=spread[:], in1=mean_sq[:])
+        nc.vector.tensor_scalar_max(out=spread[:], in0=spread[:], scalar1=EPS_STD)
+        nc.scalar.sqrt(out=v[:, HALVES : 2 * HALVES, 0:B], in_=spread[:])
+
+        nc.vector.bn_stats(out=stats[:, 0, :], in_=pooled[0:B, 0:C])
+        for q in range(HALVES, 2 * HALVES):
+            nc.tensor.transpose(
+                out=pooled[:, q * P : (q + 1) * P], in_=v[:, q, :], identity=ident[:]
+            )
+
+        nc.vector.bn_stats(out=stats[:, 1, :], in_=pooled[0:B, C : 2 * C])
+        mean_var = const.tile([B, 2], F32)
+        nc.vector.bn_aggr(out=mean_var[:], in_=stats[:])
+        sd = const.tile([B, 1], F32)
+        nc.vector.tensor_scalar_add(out=sd[:], in0=mean_var[:, 1:2], scalar1=EPS_LN)
+        nc.scalar.sqrt(out=sd[:], in_=sd[:])
+        result = const.tile([B, 2 * C], F32)
+        nc.vector.scalar_tensor_tensor(
+            out=result[:],
+            in0=pooled[0:B, :],
+            scalar=mean_var[:, 0:1],
+            in1=gain[:],
+            op0=ALU.subtract,
+            op1=ALU.mult,
+        )
+        inv_sd = const.tile([B, 1], F32)
+        nc.vector.reciprocal(out=inv_sd[:], in_=sd[:])
+        nc.vector.scalar_tensor_tensor(
+            out=result[:],
+            in0=result[:],
+            scalar=inv_sd[:],
+            in1=offset[:],
+            op0=ALU.mult,
+            op1=ALU.add,
+        )
+        nc.sync.dma_start(out=out.rearrange("b n o -> b (n o)"), in_=result[:])

@@ -39,6 +39,9 @@ EARLY_SLOTS = 7
 EARLY_FRAMES = 384
 LATE_FRAMES = 256
 GPSIMD_FRAMES = 128
+WHOLE_FROM = 8
+X_BANK = 1024
+X_BANKS = T // X_BANK
 BRIDGE_FRAMES = 208
 HEAD_FRAMES = 320
 
@@ -55,9 +58,9 @@ def tile_attentivestatspool_pb_t_kernel(
         name="feat", bufs=3
     ) as feat, tc.tile_pool(name="score", bufs=4) as score, tc.tile_pool(
         name="prod", bufs=2
-    ) as prod, tc.psum_pool(name="acc", bufs=4) as acc_pool, tc.psum_pool(
+    ) as prod, tc.psum_pool(name="acc", bufs=2) as acc_pool, tc.psum_pool(
         name="back", bufs=4
-    ) as back_pool, tc.manual_schedule():
+    ) as back_pool, tc.psum_pool(name="xp", bufs=2) as xp_pool, tc.manual_schedule():
         ident = const.tile([P, P], F32)
         make_identity(nc, ident[:])
         ident_bf = const.tile([P, P], BF16)
@@ -67,6 +70,8 @@ def tile_attentivestatspool_pb_t_kernel(
         sum_e4 = const.tile([P, HALVES, B, CHUNKS], F32)
         sum_ex = const.tile([P, HALVES, B], F32)
         sum_exx = const.tile([P, HALVES, B], F32)
+        part_ex = const.tile([P, HALVES, B - 1, X_BANKS], F32)
+        part_exx = const.tile([P, HALVES, B - 1, X_BANKS], F32)
         neg_max4 = const.tile([P, B, HALVES, CHUNKS], F32)
         neg_max = const.tile([P, B, HALVES], F32)
 
@@ -79,6 +84,7 @@ def tile_attentivestatspool_pb_t_kernel(
         first = {}
         again = {}
         x_sb = {}
+        x_bank = {}
         e = {}
         ex = {}
 
@@ -100,12 +106,17 @@ def tile_attentivestatspool_pb_t_kernel(
             src = raw[s, g][:].rearrange("p j (c i) -> p c j i", i=4)
             return dst, src
 
+        def gpsimd_frames(s):
+            if s < 2:
+                return 0
+            return GPSIMD_FRAMES if s < WHOLE_FROM else FRAMES
+
         def regroup_start(s):
             grouped[s] = grouped_pool.tile(
                 [P, PASSES, FRAMES, PACK], BF16, name="grouped", align_bytes=64
             )
             if s >= 2:
-                f = FRAMES - GPSIMD_FRAMES
+                f = FRAMES - gpsimd_frames(s)
                 nc.gpsimd.tensor_scalar(
                     out=grouped[s][:, 1, f:, :],
                     in0=raw[s, 1][:, :, f:].rearrange("p j n -> p n j"),
@@ -124,8 +135,10 @@ def tile_attentivestatspool_pb_t_kernel(
             nc.scalar.copy(out=dst[:, cut:], in_=src[:, cut:])
 
         def regroup_second_pass(s):
+            if s >= WHOLE_FROM:
+                return
             dst, src = views(s, 1)
-            end = (FRAMES - (GPSIMD_FRAMES if s >= 2 else 0)) // 4
+            end = (FRAMES - gpsimd_frames(s)) // 4
             cut = (EARLY_FRAMES if s < EARLY_SLOTS else LATE_FRAMES) // 4
             nc.vector.tensor_copy(out=dst[:, 0:cut], in_=src[:, 0:cut])
             if bridge(s):
@@ -222,13 +235,50 @@ def tile_attentivestatspool_pb_t_kernel(
                 accum_out=sum_e4[:, hf, b, c : c + 1],
             )
 
+        def features(step):
+            n = step - PRODUCT_LAG
+            if n < 0 or n % 2 or n >= 2 * HALVES * (B - 1):
+                return
+            b, hf = divmod(n // 2, HALVES)
+            for u in range(X_BANKS):
+                x_bank[b, hf, u] = xp_pool.tile([P, X_BANK], BF16, name="x_bank")
+                for i in range(X_BANK // FRAMES):
+                    at = u * X_BANK + i * FRAMES
+                    nc.tensor.matmul(
+                        out=x_bank[b, hf, u][:, i * FRAMES : (i + 1) * FRAMES],
+                        lhsT=ident_bf[:],
+                        rhs=x_sb[b][:, hf, at : at + FRAMES],
+                        start=True,
+                        stop=True,
+                    )
+
+        def product_banks(b, hf, second):
+            out_tile = prod.tile([P, T], F32, name="exx" if second else "ex")
+            in_tile = ex[b, hf] if second else e[b, hf]
+            sums = part_exx if second else part_ex
+            if not second:
+                ex[b, hf] = out_tile
+            for u in range(X_BANKS):
+                cols = slice(u * X_BANK, (u + 1) * X_BANK)
+                nc.vector.scalar_tensor_tensor(
+                    out=out_tile[:, cols],
+                    in0=in_tile[:, cols],
+                    scalar=1.0,
+                    in1=x_bank[b, hf, u][:],
+                    op0=ALU.mult,
+                    op1=ALU.mult,
+                    accum_out=sums[:, hf, b, u : u + 1],
+                )
+
         def product(step):
             n = step - PRODUCT_LAG
             if n < 0 or n >= 2 * HALVES * B:
                 return
             b, k = divmod(n, 2 * HALVES)
             hf, second = divmod(k, 2)
-            if not second:
+            if b < B - 1:
+                product_banks(b, hf, second)
+            elif not second:
                 ex[b, hf] = prod.tile([P, T], F32, name="ex")
                 nc.vector.scalar_tensor_tensor(
                     out=ex[b, hf][:],
@@ -302,6 +352,7 @@ def tile_attentivestatspool_pb_t_kernel(
                 nc.sync.dma_start(out=gain[:], in_=g2.partition_broadcast(B))
                 nc.sync.dma_start(out=offset[:], in_=be2.partition_broadcast(B))
             now = units(step)
+            features(step)
             if step < SLOTS:
                 quantise(step)
                 multiply(step)
@@ -334,6 +385,12 @@ def tile_attentivestatspool_pb_t_kernel(
             if step == STEPS - 1:
                 pooled = back_pool.tile([P, 2 * C], F32, name="back")
                 sum_e = const.tile([P, HALVES, B], F32)
+                nc.vector.tensor_reduce(
+                    out=sum_ex[:, :, 0 : B - 1], in_=part_ex[:], axis=AX.X, op=ALU.add
+                )
+                nc.vector.tensor_reduce(
+                    out=sum_exx[:, :, 0 : B - 1], in_=part_exx[:], axis=AX.X, op=ALU.add
+                )
                 nc.vector.tensor_reduce(out=sum_e[:], in_=sum_e4[:], axis=AX.X, op=ALU.add)
                 nc.vector.reciprocal(out=inv_e[:], in_=sum_e[:])
                 nc.vector.tensor_mul(out=v[:, 0:HALVES, 0:B], in0=sum_ex[:], in1=inv_e[:])

@@ -32,17 +32,18 @@ MASKED = 1.0e30
 
 SLOTS = B * CHUNKS
 LOAD_AHEAD = 3
-EXP_LAG = 4
-PRODUCT_LAG = 6
+PARTS = 2
+PART_SLOTS = CHUNKS // PARTS
+PART = T // PARTS
+GROUPS = B * PARTS
+EXP_LAG = PART_SLOTS
+PRODUCT_LAG = PART_SLOTS + 1
 STEPS = SLOTS + PRODUCT_LAG
-EARLY_SLOTS = 7
 EARLY_FRAMES = 384
-LATE_FRAMES = 256
 GPSIMD_FRAMES = 128
-WHOLE_FROM = 8
-X_BANK = 1024
-X_BANKS = T // X_BANK
-BRIDGE_FRAMES = 208
+WHOLE_FROM = 5
+EXTRA_FROM = 6
+EXTRA_FRAMES = 64
 HEAD_FRAMES = 320
 
 
@@ -68,12 +69,10 @@ def tile_attentivestatspool_pb_t_kernel(
         v = const.tile([P, 2 * HALVES, P], F32)
         nc.gpsimd.memset(v[:], 0.0)
         sum_e4 = const.tile([P, HALVES, B, CHUNKS], F32)
-        sum_ex = const.tile([P, HALVES, B], F32)
-        sum_exx = const.tile([P, HALVES, B], F32)
-        part_ex = const.tile([P, HALVES, B - 1, X_BANKS], F32)
-        part_exx = const.tile([P, HALVES, B - 1, X_BANKS], F32)
-        neg_max4 = const.tile([P, B, HALVES, CHUNKS], F32)
-        neg_max = const.tile([P, B, HALVES], F32)
+        part_ex = const.tile([P, PARTS, HALVES, B], F32)
+        part_exx = const.tile([P, PARTS, HALVES, B], F32)
+        neg_max4 = const.tile([P, HALVES, B, CHUNKS], F32)
+        neg_max = const.tile([P, PARTS, HALVES, B], F32)
 
         raw = {}
         grouped = {}
@@ -111,43 +110,46 @@ def tile_attentivestatspool_pb_t_kernel(
                 return 0
             return GPSIMD_FRAMES if s < WHOLE_FROM else FRAMES
 
+        def gpsimd_copy(s, g, f):
+            nc.gpsimd.tensor_scalar(
+                out=grouped[s][:, g, f:, :],
+                in0=raw[s, g][:, :, f:].rearrange("p j n -> p n j"),
+                scalar1=1.0,
+                scalar2=0.0,
+                op0=ALU.mult,
+                op1=ALU.add,
+            )
+
         def regroup_start(s):
             grouped[s] = grouped_pool.tile(
                 [P, PASSES, FRAMES, PACK], BF16, name="grouped", align_bytes=64
             )
             if s >= 2:
                 f = FRAMES - gpsimd_frames(s)
-                nc.gpsimd.tensor_scalar(
-                    out=grouped[s][:, 1, f:, :],
-                    in0=raw[s, 1][:, :, f:].rearrange("p j n -> p n j"),
-                    scalar1=1.0,
-                    scalar2=0.0,
-                    op0=ALU.mult,
-                    op1=ALU.add,
-                )
-
-        def bridge(s):
-            return EXP_LAG < s < EARLY_SLOTS
+                gpsimd_copy(s, 1, f)
+            if s >= EXTRA_FROM:
+                gpsimd_copy(s, 0, FRAMES - EXTRA_FRAMES)
 
         def regroup_first_pass(s):
             dst, src = views(s, 0)
-            cut = (BRIDGE_FRAMES if bridge(s) else 0) // 4
-            nc.scalar.copy(out=dst[:, cut:], in_=src[:, cut:])
+            end = (FRAMES - (EXTRA_FRAMES if s >= EXTRA_FROM else 0)) // 4
+            nc.scalar.copy(out=dst[:, 0:end], in_=src[:, 0:end])
 
         def regroup_second_pass(s):
             if s >= WHOLE_FROM:
                 return
             dst, src = views(s, 1)
             end = (FRAMES - gpsimd_frames(s)) // 4
-            cut = (EARLY_FRAMES if s < EARLY_SLOTS else LATE_FRAMES) // 4
-            nc.vector.tensor_copy(out=dst[:, 0:cut], in_=src[:, 0:cut])
-            if bridge(s):
-                dst0, src0 = views(s, 0)
-                nc.vector.tensor_copy(
-                    out=dst0[:, 0 : BRIDGE_FRAMES // 4], in_=src0[:, 0 : BRIDGE_FRAMES // 4]
-                )
+            cut = EARLY_FRAMES // 4
             if cut < end:
                 nc.scalar.copy(out=dst[:, cut:end], in_=src[:, cut:end])
+
+        def regroup_vector(s):
+            if s >= WHOLE_FROM:
+                return
+            dst, src = views(s, 1)
+            cut = EARLY_FRAMES // 4
+            nc.vector.tensor_copy(out=dst[:, 0:cut], in_=src[:, 0:cut])
 
         def quantise(s):
             codes[s] = quant.tile([P, PASSES * FRAMES], U32, name="codes", align_bytes=64)
@@ -204,102 +206,81 @@ def tile_attentivestatspool_pb_t_kernel(
             b, c = divmod(s, CHUNKS)
             for hf in range(HALVES):
                 nc.vector.tensor_reduce(
-                    out=neg_max4[:, b, hf, c : c + 1],
+                    out=neg_max4[:, hf, b, c : c + 1],
                     in_=first[s, hf][:],
                     axis=AX.X,
                     op=ALU.max,
                     negate=True,
                 )
-            if c == CHUNKS - 1:
+
+        def part_max(s):
+            b, c = divmod(s, CHUNKS)
+            part, last = divmod(c, PART_SLOTS)
+            if last == PART_SLOTS - 1:
                 nc.vector.tensor_reduce(
-                    out=neg_max[:, b, :], in_=neg_max4[:, b], axis=AX.X, op=ALU.min
+                    out=neg_max[:, part, :, b : b + 1],
+                    in_=neg_max4[:, :, b, 0 : c + 1],
+                    axis=AX.X,
+                    op=ALU.min,
                 )
 
         def units(step):
-            found = []
-            for b in range(B):
-                k = 2 * (step - CHUNKS * b - EXP_LAG)
-                if 0 <= k < HALVES * CHUNKS:
-                    found.extend([(b, n % CHUNKS, n // CHUNKS) for n in (k, k + 1)])
-            return found
+            group, hf = divmod(step - EXP_LAG, HALVES)
+            if not 0 <= group < GROUPS:
+                return []
+            b, part = divmod(group, PARTS)
+            return [(b, part * PART_SLOTS + n, hf) for n in range(PART_SLOTS)]
 
         def exponent(b, c, hf):
-            if c == 0:
-                e[b, hf] = score.tile([P, T], F32, name="e")
+            part, n = divmod(c, PART_SLOTS)
+            if n == 0:
+                e[b, part, hf] = score.tile([P, PART], F32, name="e")
             nc.scalar.activation(
-                out=e[b, hf][:, c * FRAMES : (c + 1) * FRAMES],
+                out=e[b, part, hf][:, n * FRAMES : (n + 1) * FRAMES],
                 in_=again[b, c, hf][:],
                 func=ACT.Exp,
-                bias=neg_max[:, b, hf : hf + 1],
+                bias=neg_max[:, part, hf, b : b + 1],
                 scale=1.0,
                 accum_out=sum_e4[:, hf, b, c : c + 1],
             )
 
-        def features(step):
-            n = step - PRODUCT_LAG
-            if n < 0 or n % 2 or n >= 2 * HALVES * (B - 1):
-                return
-            b, hf = divmod(n // 2, HALVES)
-            for u in range(X_BANKS):
-                x_bank[b, hf, u] = xp_pool.tile([P, X_BANK], BF16, name="x_bank")
-                for i in range(X_BANK // FRAMES):
-                    at = u * X_BANK + i * FRAMES
-                    nc.tensor.matmul(
-                        out=x_bank[b, hf, u][:, i * FRAMES : (i + 1) * FRAMES],
-                        lhsT=ident_bf[:],
-                        rhs=x_sb[b][:, hf, at : at + FRAMES],
-                        start=True,
-                        stop=True,
-                    )
+        def place(n):
+            group, hf = divmod(n, HALVES)
+            b, part = divmod(group, PARTS)
+            return b, part, hf
 
-        def product_banks(b, hf, second):
-            out_tile = prod.tile([P, T], F32, name="exx" if second else "ex")
-            in_tile = ex[b, hf] if second else e[b, hf]
-            sums = part_exx if second else part_ex
+        def features(n):
+            b, part, hf = place(n)
+            if b == B - 1:
+                return
+            bank = xp_pool.tile([P, PART], BF16, name="x_bank")
+            x_bank[n] = bank
+            for i in range(PART // FRAMES):
+                at = part * PART + i * FRAMES
+                nc.tensor.matmul(
+                    out=bank[:, i * FRAMES : (i + 1) * FRAMES],
+                    lhsT=ident_bf[:],
+                    rhs=x_sb[b][:, hf, at : at + FRAMES],
+                    start=True,
+                    stop=True,
+                )
+
+        def product(n, second):
+            b, part, hf = place(n)
+            result = prod.tile([P, PART], F32, name="exx" if second else "ex")
             if not second:
-                ex[b, hf] = out_tile
-            for u in range(X_BANKS):
-                cols = slice(u * X_BANK, (u + 1) * X_BANK)
-                nc.vector.scalar_tensor_tensor(
-                    out=out_tile[:, cols],
-                    in0=in_tile[:, cols],
-                    scalar=1.0,
-                    in1=x_bank[b, hf, u][:],
-                    op0=ALU.mult,
-                    op1=ALU.mult,
-                    accum_out=sums[:, hf, b, u : u + 1],
-                )
-
-        def product(step):
-            n = step - PRODUCT_LAG
-            if n < 0 or n >= 2 * HALVES * B:
-                return
-            b, k = divmod(n, 2 * HALVES)
-            hf, second = divmod(k, 2)
-            if b < B - 1:
-                product_banks(b, hf, second)
-            elif not second:
-                ex[b, hf] = prod.tile([P, T], F32, name="ex")
-                nc.vector.scalar_tensor_tensor(
-                    out=ex[b, hf][:],
-                    in0=e[b, hf][:],
-                    scalar=1.0,
-                    in1=x_sb[b][:, hf, :],
-                    op0=ALU.mult,
-                    op1=ALU.mult,
-                    accum_out=sum_ex[:, hf, b : b + 1],
-                )
-            else:
-                exx = prod.tile([P, T], F32, name="exx")
-                nc.vector.scalar_tensor_tensor(
-                    out=exx[:],
-                    in0=ex[b, hf][:],
-                    scalar=1.0,
-                    in1=x_sb[b][:, hf, :],
-                    op0=ALU.mult,
-                    op1=ALU.mult,
-                    accum_out=sum_exx[:, hf, b : b + 1],
-                )
+                ex[n] = result
+            nc.vector.scalar_tensor_tensor(
+                out=result[:],
+                in0=(ex[n] if second else e[b, part, hf])[:],
+                scalar=1.0,
+                in1=x_bank[n][:]
+                if b < B - 1
+                else x_sb[b][:, hf, part * PART : (part + 1) * PART],
+                op0=ALU.mult,
+                op1=ALU.mult,
+                accum_out=(part_exx if second else part_ex)[:, part, hf, b : b + 1],
+            )
 
         load(0)
         load(1)
@@ -338,6 +319,15 @@ def tile_attentivestatspool_pb_t_kernel(
         regroup_start(1)
 
         warm = const.tile([P, 1], F32)
+        eps_ln = const.tile([P, 1], F32)
+        nc.vector.tensor_scalar(
+            out=eps_ln[:],
+            in0=ident[:, 0:1],
+            scalar1=0.0,
+            scalar2=EPS_LN,
+            op0=ALU.mult,
+            op1=ALU.add,
+        )
         inv_e = const.tile([P, HALVES, B], F32)
         mean_sq = const.tile([P, HALVES, B], F32)
         gain = const.tile([B, 2 * C], BF16)
@@ -346,13 +336,15 @@ def tile_attentivestatspool_pb_t_kernel(
         for step in range(STEPS):
             if step + LOAD_AHEAD < SLOTS:
                 load(step + LOAD_AHEAD)
-            if step < SLOTS and step % CHUNKS == CHUNKS - 1:
+            if step < SLOTS and step % CHUNKS == 0:
                 load_x(step // CHUNKS)
             if step == SLOTS - 1:
                 nc.sync.dma_start(out=gain[:], in_=g2.partition_broadcast(B))
                 nc.sync.dma_start(out=offset[:], in_=be2.partition_broadcast(B))
             now = units(step)
-            features(step)
+            now_first = step - PRODUCT_LAG
+            if 0 <= now_first < HALVES * GROUPS:
+                features(now_first)
             if step < SLOTS:
                 quantise(step)
                 multiply(step)
@@ -371,6 +363,18 @@ def tile_attentivestatspool_pb_t_kernel(
                 regroup_start(step + 2)
             if 1 <= step <= SLOTS:
                 chunk_max(step - 1)
+            if 1 <= now_first <= SLOTS - PRODUCT_LAG:
+                product(now_first - 1, True)
+            if 1 <= step <= SLOTS:
+                part_max(step - 1)
+            copy_first = step + 2 < WHOLE_FROM
+            if step + 1 < SLOTS and copy_first:
+                regroup_vector(step + 1)
+            if step < SLOTS:
+                if 0 <= now_first:
+                    product(now_first, False)
+                if step + 1 < SLOTS and not copy_first:
+                    regroup_vector(step + 1)
             if step + 1 < SLOTS:
                 regroup_first_pass(step + 1)
                 regroup_second_pass(step + 1)
@@ -380,32 +384,48 @@ def tile_attentivestatspool_pb_t_kernel(
                     first[step, hf] = turn(step // CHUNKS, step % CHUNKS, hf)
             for b, c, hf in now:
                 exponent(b, c, hf)
-            if step == CHUNKS * (B - 1) + EXP_LAG + CHUNKS - 1:
-                nc.scalar.sqrt(out=warm[:], in_=ident[:, 0:1])
-            if step == STEPS - 1:
-                pooled = back_pool.tile([P, 2 * C], F32, name="back")
-                sum_e = const.tile([P, HALVES, B], F32)
-                nc.vector.tensor_reduce(
-                    out=sum_ex[:, :, 0 : B - 1], in_=part_ex[:], axis=AX.X, op=ALU.add
-                )
-                nc.vector.tensor_reduce(
-                    out=sum_exx[:, :, 0 : B - 1], in_=part_exx[:], axis=AX.X, op=ALU.add
-                )
-                nc.vector.tensor_reduce(out=sum_e[:], in_=sum_e4[:], axis=AX.X, op=ALU.add)
-                nc.vector.reciprocal(out=inv_e[:], in_=sum_e[:])
-                nc.vector.tensor_mul(out=v[:, 0:HALVES, 0:B], in0=sum_ex[:], in1=inv_e[:])
-                nc.vector.tensor_mul(
-                    out=mean_sq[:], in0=v[:, 0:HALVES, 0:B], in1=v[:, 0:HALVES, 0:B]
-                )
-                for q in range(HALVES):
-                    nc.tensor.transpose(
-                        out=pooled[:, q * P : (q + 1) * P], in_=v[:, q, :], identity=ident[:]
-                    )
-            product(step)
+
+        n = SLOTS - PRODUCT_LAG
+        weight = const.tile([P, HALVES, B], F32)
+        sum_e2 = const.tile([P, HALVES, B, PARTS], F32)
+        sum_e = const.tile([P, HALVES, B], F32)
+        sum_x = const.tile([P, HALVES, B], F32)
+        base = const.tile([P, HALVES, B], F32)
+        mean = v[:, 0:HALVES, 0:B]
+        nc.vector.tensor_sub(out=weight[:], in0=neg_max[:, 1], in1=neg_max[:, 0])
+        nc.scalar.activation(out=weight[:], in_=weight[:], func=ACT.Exp)
+        nc.scalar.sqrt(out=warm[:], in_=ident[:, 0:1])
+        product(n, False)
+        product(n + 1, False)
+        nc.vector.tensor_reduce(
+            out=sum_e2[:],
+            in_=sum_e4[:].rearrange("p h b (i c) -> p h b i c", i=PARTS),
+            axis=AX.X,
+            op=ALU.add,
+        )
+        nc.vector.tensor_mul(out=sum_x[:], in0=part_ex[:, 0], in1=weight[:])
+        product(n, True)
+        nc.vector.tensor_mul(out=sum_e[:], in0=sum_e2[:, :, :, 0], in1=weight[:])
+        nc.vector.tensor_mul(out=base[:], in0=part_exx[:, 0], in1=weight[:])
+        product(n + 2, False)
+        nc.vector.tensor_add(out=sum_e[:], in0=sum_e[:], in1=sum_e2[:, :, :, 1])
+        nc.vector.tensor_add(out=sum_x[:], in0=sum_x[:], in1=part_ex[:, 1])
+        nc.vector.reciprocal(out=inv_e[:], in_=sum_e[:])
+        product(n + 1, True)
+        nc.vector.tensor_mul(out=mean, in0=sum_x[:], in1=inv_e[:])
+        nc.vector.tensor_mul(out=base[:], in0=base[:], in1=inv_e[:])
+        pooled = back_pool.tile([P, 2 * C], F32, name="back")
+        for q in range(HALVES):
+            nc.tensor.transpose(
+                out=pooled[:, q * P : (q + 1) * P], in_=v[:, q, :], identity=ident[:]
+            )
+        nc.vector.tensor_mul(out=mean_sq[:], in0=mean, in1=mean)
+        product(n + 2, True)
 
         spread = const.tile([P, HALVES, B], F32)
-        nc.vector.tensor_mul(out=spread[:], in0=sum_exx[:], in1=inv_e[:])
-        nc.vector.tensor_sub(out=spread[:], in0=spread[:], in1=mean_sq[:])
+        nc.vector.tensor_mul(out=spread[:], in0=part_exx[:, 1], in1=inv_e[:])
+        nc.vector.tensor_sub(out=base[:], in0=base[:], in1=mean_sq[:])
+        nc.vector.tensor_add(out=spread[:], in0=spread[:], in1=base[:])
         nc.vector.tensor_scalar_max(out=spread[:], in0=spread[:], scalar1=EPS_STD)
         nc.scalar.sqrt(out=v[:, HALVES : 2 * HALVES, 0:B], in_=spread[:])
 
@@ -419,8 +439,9 @@ def tile_attentivestatspool_pb_t_kernel(
         mean_var = const.tile([B, 2], F32)
         nc.vector.bn_aggr(out=mean_var[:], in_=stats[:])
         sd = const.tile([B, 1], F32)
-        nc.vector.tensor_scalar_add(out=sd[:], in0=mean_var[:, 1:2], scalar1=EPS_LN)
-        nc.scalar.sqrt(out=sd[:], in_=sd[:])
+        nc.scalar.activation(
+            out=sd[:], in_=mean_var[:, 1:2], func=ACT.Sqrt, bias=eps_ln[0:B, :], scale=1.0
+        )
         result = const.tile([B, 2 * C], F32)
         nc.vector.scalar_tensor_tensor(
             out=result[:],

@@ -39,10 +39,10 @@ GROUPS = B * PARTS
 EXP_LAG = PART_SLOTS
 PRODUCT_LAG = PART_SLOTS + 1
 STEPS = SLOTS + PRODUCT_LAG
-EARLY_FRAMES = 384
+EARLY_FRAMES = (64, 384)
 GPSIMD_FRAMES = 128
-WHOLE_FROM = 5
-EXTRA_FROM = 6
+WHOLE_FROM = 6
+EXTRA_FROM = 7
 EXTRA_FRAMES = 64
 HEAD_FRAMES = 320
 
@@ -133,23 +133,25 @@ def tile_attentivestatspool_pb_t_kernel(
         def regroup_first_pass(s):
             dst, src = views(s, 0)
             end = (FRAMES - (EXTRA_FRAMES if s >= EXTRA_FROM else 0)) // 4
-            nc.scalar.copy(out=dst[:, 0:end], in_=src[:, 0:end])
+            cut = (EARLY_FRAMES[0] if s < WHOLE_FROM else 0) // 4
+            nc.scalar.copy(out=dst[:, cut:end], in_=src[:, cut:end])
 
         def regroup_second_pass(s):
             if s >= WHOLE_FROM:
                 return
             dst, src = views(s, 1)
             end = (FRAMES - gpsimd_frames(s)) // 4
-            cut = EARLY_FRAMES // 4
+            cut = EARLY_FRAMES[1] // 4
             if cut < end:
                 nc.scalar.copy(out=dst[:, cut:end], in_=src[:, cut:end])
 
         def regroup_vector(s):
             if s >= WHOLE_FROM:
                 return
-            dst, src = views(s, 1)
-            cut = EARLY_FRAMES // 4
-            nc.vector.tensor_copy(out=dst[:, 0:cut], in_=src[:, 0:cut])
+            for g in range(PASSES):
+                dst, src = views(s, g)
+                cut = EARLY_FRAMES[g] // 4
+                nc.vector.tensor_copy(out=dst[:, 0:cut], in_=src[:, 0:cut])
 
         def quantise(s):
             codes[s] = quant.tile([P, PASSES * FRAMES], U32, name="codes", align_bytes=64)
@@ -158,6 +160,17 @@ def tile_attentivestatspool_pb_t_kernel(
                 out=codes[s][:].bitcast(FP8X4),
                 scales=planes[s][:],
                 in_=grouped[s][:].rearrange("p g n j -> p (g n j)"),
+            )
+
+        def quantise_pass(s, g):
+            if g == 0:
+                codes[s] = quant.tile([P, PASSES * FRAMES], U32, name="codes", align_bytes=64)
+                planes[s] = quant.tile([P, PASSES * FRAMES], U8, name="planes", align_bytes=64)
+            cols = slice(g * FRAMES, (g + 1) * FRAMES)
+            nc.vector.quantize_mx(
+                out=codes[s][:, cols].bitcast(FP8X4),
+                scales=planes[s][:, cols],
+                in_=grouped[s][:, g].rearrange("p n j -> p (n j)"),
             )
 
         def multiply(s):
@@ -306,6 +319,8 @@ def tile_attentivestatspool_pb_t_kernel(
             )
         for s in range(2, LOAD_AHEAD):
             load(s)
+        warm = const.tile([P, 1], F32)
+        nc.scalar.activation(out=warm[:], in_=ident[:, 0:1], func=ACT.Exp)
         mask_cols = back_pool.tile([P, P], BF16, name="back")
         nc.tensor.transpose(out=mask_cols[:], in_=mask_rows[:], identity=ident_bf[:])
         penalty = const.tile([P, B * UTT_TILES], F32)
@@ -316,9 +331,9 @@ def tile_attentivestatspool_pb_t_kernel(
                 out=dst[:, 0 : HEAD_FRAMES // 4], in_=src[:, 0 : HEAD_FRAMES // 4]
             )
             nc.scalar.copy(out=dst[:, HEAD_FRAMES // 4 :], in_=src[:, HEAD_FRAMES // 4 :])
+            quantise_pass(0, g)
         regroup_start(1)
 
-        warm = const.tile([P, 1], F32)
         eps_ln = const.tile([P, 1], F32)
         nc.vector.tensor_scalar(
             out=eps_ln[:],
@@ -336,7 +351,7 @@ def tile_attentivestatspool_pb_t_kernel(
         for step in range(STEPS):
             if step + LOAD_AHEAD < SLOTS:
                 load(step + LOAD_AHEAD)
-            if step < SLOTS and step % CHUNKS == 0:
+            if step < SLOTS and step % CHUNKS == 1:
                 load_x(step // CHUNKS)
             if step == SLOTS - 1:
                 nc.sync.dma_start(out=gain[:], in_=g2.partition_broadcast(B))
@@ -346,10 +361,13 @@ def tile_attentivestatspool_pb_t_kernel(
             if 0 <= now_first < HALVES * GROUPS:
                 features(now_first)
             if step < SLOTS:
-                quantise(step)
+                if step > 0:
+                    quantise(step)
                 multiply(step)
             for b, c, hf in now:
                 again[b, c, hf] = turn(b, c, hf)
+            if step + 1 < SLOTS:
+                regroup_vector(step + 1)
             if step == 0:
                 nc.vector.tensor_scalar(
                     out=penalty[:],
@@ -367,14 +385,8 @@ def tile_attentivestatspool_pb_t_kernel(
                 product(now_first - 1, True)
             if 1 <= step <= SLOTS:
                 part_max(step - 1)
-            copy_first = step + 2 < WHOLE_FROM
-            if step + 1 < SLOTS and copy_first:
-                regroup_vector(step + 1)
-            if step < SLOTS:
-                if 0 <= now_first:
-                    product(now_first, False)
-                if step + 1 < SLOTS and not copy_first:
-                    regroup_vector(step + 1)
+            if step < SLOTS and 0 <= now_first:
+                product(now_first, False)
             if step + 1 < SLOTS:
                 regroup_first_pass(step + 1)
                 regroup_second_pass(step + 1)

@@ -39,8 +39,12 @@ GROUPS = B * PARTS
 EXP_LAG = PART_SLOTS
 PRODUCT_LAG = PART_SLOTS + 1
 STEPS = SLOTS + PRODUCT_LAG
-EARLY_FRAMES = (64, 384)
+EARLY_FRAMES = (32, 384)
+GPSIMD_PRODUCTS = (11,)
 GPSIMD_FRAMES = 128
+BRIDGE_SLOT = 5
+BRIDGE_FRAMES = (0, 64)
+BRIDGE_GPSIMD_FRAMES = 384
 WHOLE_FROM = 6
 EXTRA_FROM = 7
 EXTRA_FRAMES = 64
@@ -56,7 +60,7 @@ def tile_attentivestatspool_pb_t_kernel(
     ) as raw_pool, tc.tile_pool(name="grouped", bufs=2) as grouped_pool, tc.tile_pool(
         name="quant", bufs=3
     ) as quant, tc.tile_pool(name="turned", bufs=2) as turned_pool, tc.tile_pool(
-        name="feat", bufs=3
+        name="feat", bufs=5
     ) as feat, tc.tile_pool(name="score", bufs=4) as score, tc.tile_pool(
         name="prod", bufs=2
     ) as prod, tc.psum_pool(name="acc", bufs=2) as acc_pool, tc.psum_pool(
@@ -96,9 +100,15 @@ def tile_attentivestatspool_pb_t_kernel(
                     out=raw[s, g][:], in_=h_rows[g, :, :, c * FRAMES : (c + 1) * FRAMES]
                 )
 
-        def load_x(b):
-            x_sb[b] = feat.tile([P, HALVES, T], BF16, name="x_sb")
-            nc.sync.dma_start(out=x_sb[b][:], in_=x[b].rearrange("(hf p) n -> p hf n", p=P))
+        def load_x(group):
+            b, part = divmod(group, PARTS)
+            x_sb[group] = feat.tile([P, HALVES, PART], BF16, name="x_sb")
+            nc.sync.dma_start(
+                out=x_sb[group][:],
+                in_=x[b].rearrange("(hf p) n -> p hf n", p=P)[
+                    :, :, part * PART : (part + 1) * PART
+                ],
+            )
 
         def views(s, g):
             dst = grouped[s][:, g].rearrange("p (c i) j -> p c j i", i=4)
@@ -108,7 +118,14 @@ def tile_attentivestatspool_pb_t_kernel(
         def gpsimd_frames(s):
             if s < 2:
                 return 0
-            return GPSIMD_FRAMES if s < WHOLE_FROM else FRAMES
+            if s < WHOLE_FROM:
+                return BRIDGE_GPSIMD_FRAMES if s == BRIDGE_SLOT else GPSIMD_FRAMES
+            return FRAMES
+
+        def vector_frames(s):
+            if s >= WHOLE_FROM:
+                return (0, 0)
+            return BRIDGE_FRAMES if s == BRIDGE_SLOT else EARLY_FRAMES
 
         def gpsimd_copy(s, g, f):
             nc.gpsimd.tensor_scalar(
@@ -133,7 +150,7 @@ def tile_attentivestatspool_pb_t_kernel(
         def regroup_first_pass(s):
             dst, src = views(s, 0)
             end = (FRAMES - (EXTRA_FRAMES if s >= EXTRA_FROM else 0)) // 4
-            cut = (EARLY_FRAMES[0] if s < WHOLE_FROM else 0) // 4
+            cut = vector_frames(s)[0] // 4
             nc.scalar.copy(out=dst[:, cut:end], in_=src[:, cut:end])
 
         def regroup_second_pass(s):
@@ -141,7 +158,7 @@ def tile_attentivestatspool_pb_t_kernel(
                 return
             dst, src = views(s, 1)
             end = (FRAMES - gpsimd_frames(s)) // 4
-            cut = EARLY_FRAMES[1] // 4
+            cut = vector_frames(s)[1] // 4
             if cut < end:
                 nc.scalar.copy(out=dst[:, cut:end], in_=src[:, cut:end])
 
@@ -150,8 +167,9 @@ def tile_attentivestatspool_pb_t_kernel(
                 return
             for g in range(PASSES):
                 dst, src = views(s, g)
-                cut = EARLY_FRAMES[g] // 4
-                nc.vector.tensor_copy(out=dst[:, 0:cut], in_=src[:, 0:cut])
+                cut = vector_frames(s)[g] // 4
+                if cut > 0:
+                    nc.vector.tensor_copy(out=dst[:, 0:cut], in_=src[:, 0:cut])
 
         def quantise(s):
             codes[s] = quant.tile([P, PASSES * FRAMES], U32, name="codes", align_bytes=64)
@@ -262,21 +280,44 @@ def tile_attentivestatspool_pb_t_kernel(
             b, part = divmod(group, PARTS)
             return b, part, hf
 
+        def in_psum(n):
+            return n < 11 or n == 13
+
         def features(n):
-            b, part, hf = place(n)
-            if b == B - 1:
+            if not in_psum(n):
                 return
+            b, part, hf = place(n)
             bank = xp_pool.tile([P, PART], BF16, name="x_bank")
             x_bank[n] = bank
             for i in range(PART // FRAMES):
-                at = part * PART + i * FRAMES
+                at = i * FRAMES
                 nc.tensor.matmul(
                     out=bank[:, i * FRAMES : (i + 1) * FRAMES],
                     lhsT=ident_bf[:],
-                    rhs=x_sb[b][:, hf, at : at + FRAMES],
+                    rhs=x_sb[n // HALVES][:, hf, at : at + FRAMES],
                     start=True,
                     stop=True,
                 )
+
+        def gpsimd_product(n):
+            b, part, hf = place(n)
+            ex[n] = prod.tile([P, PART], F32, name="ex")
+            nc.gpsimd.tensor_tensor(
+                out=ex[n][:],
+                in0=e[b, part, hf][:],
+                in1=x_sb[n // HALVES][:, hf, :],
+                op=ALU.mult,
+            )
+
+        def gpsimd_sum(n):
+            b, part, hf = place(n)
+            spare = score.tile([P, PART], F32, name="spare")
+            nc.scalar.activation(
+                out=spare[:],
+                in_=ex[n][:],
+                func=ACT.Copy,
+                accum_out=part_ex[:, part, hf, b : b + 1],
+            )
 
         def product(n, second):
             b, part, hf = place(n)
@@ -288,8 +329,8 @@ def tile_attentivestatspool_pb_t_kernel(
                 in0=(ex[n] if second else e[b, part, hf])[:],
                 scalar=1.0,
                 in1=x_bank[n][:]
-                if b < B - 1
-                else x_sb[b][:, hf, part * PART : (part + 1) * PART],
+                if in_psum(n)
+                else x_sb[n // HALVES][:, hf, :],
                 op0=ALU.mult,
                 op1=ALU.mult,
                 accum_out=(part_exx if second else part_ex)[:, part, hf, b : b + 1],
@@ -351,8 +392,8 @@ def tile_attentivestatspool_pb_t_kernel(
         for step in range(STEPS):
             if step + LOAD_AHEAD < SLOTS:
                 load(step + LOAD_AHEAD)
-            if step < SLOTS and step % CHUNKS == 1:
-                load_x(step // CHUNKS)
+            if step < SLOTS and step % PART_SLOTS == 1:
+                load_x(step // PART_SLOTS)
             if step == SLOTS - 1:
                 nc.sync.dma_start(out=gain[:], in_=g2.partition_broadcast(B))
                 nc.sync.dma_start(out=offset[:], in_=be2.partition_broadcast(B))
@@ -381,12 +422,17 @@ def tile_attentivestatspool_pb_t_kernel(
                 regroup_start(step + 2)
             if 1 <= step <= SLOTS:
                 chunk_max(step - 1)
+            if step == SLOTS:
+                part_max(step - 1)
             if 1 <= now_first <= SLOTS - PRODUCT_LAG:
                 product(now_first - 1, True)
-            if 1 <= step <= SLOTS:
+            if 1 <= step < SLOTS:
                 part_max(step - 1)
             if step < SLOTS and 0 <= now_first:
-                product(now_first, False)
+                if now_first in GPSIMD_PRODUCTS:
+                    gpsimd_product(now_first)
+                else:
+                    product(now_first, False)
             if step + 1 < SLOTS:
                 regroup_first_pass(step + 1)
                 regroup_second_pass(step + 1)
@@ -396,6 +442,8 @@ def tile_attentivestatspool_pb_t_kernel(
                     first[step, hf] = turn(step // CHUNKS, step % CHUNKS, hf)
             for b, c, hf in now:
                 exponent(b, c, hf)
+            if now_first in GPSIMD_PRODUCTS:
+                gpsimd_sum(now_first)
 
         n = SLOTS - PRODUCT_LAG
         weight = const.tile([P, HALVES, B], F32)
@@ -404,11 +452,13 @@ def tile_attentivestatspool_pb_t_kernel(
         sum_x = const.tile([P, HALVES, B], F32)
         base = const.tile([P, HALVES, B], F32)
         mean = v[:, 0:HALVES, 0:B]
+        product(n, False)
         nc.vector.tensor_sub(out=weight[:], in0=neg_max[:, 1], in1=neg_max[:, 0])
         nc.scalar.activation(out=weight[:], in_=weight[:], func=ACT.Exp)
         nc.scalar.sqrt(out=warm[:], in_=ident[:, 0:1])
-        product(n, False)
-        product(n + 1, False)
+        gpsimd_product(n + 1)
+        gpsimd_sum(n + 1)
+        product(n, True)
         nc.vector.tensor_reduce(
             out=sum_e2[:],
             in_=sum_e4[:].rearrange("p h b (i c) -> p h b i c", i=PARTS),
@@ -416,23 +466,22 @@ def tile_attentivestatspool_pb_t_kernel(
             op=ALU.add,
         )
         nc.vector.tensor_mul(out=sum_x[:], in0=part_ex[:, 0], in1=weight[:])
-        product(n, True)
+        product(n + 2, False)
         nc.vector.tensor_mul(out=sum_e[:], in0=sum_e2[:, :, :, 0], in1=weight[:])
         nc.vector.tensor_mul(out=base[:], in0=part_exx[:, 0], in1=weight[:])
-        product(n + 2, False)
         nc.vector.tensor_add(out=sum_e[:], in0=sum_e[:], in1=sum_e2[:, :, :, 1])
-        nc.vector.tensor_add(out=sum_x[:], in0=sum_x[:], in1=part_ex[:, 1])
-        nc.vector.reciprocal(out=inv_e[:], in_=sum_e[:])
         product(n + 1, True)
-        nc.vector.tensor_mul(out=mean, in0=sum_x[:], in1=inv_e[:])
+        nc.vector.reciprocal(out=inv_e[:], in_=sum_e[:])
+        nc.vector.tensor_add(out=sum_x[:], in0=sum_x[:], in1=part_ex[:, 1])
         nc.vector.tensor_mul(out=base[:], in0=base[:], in1=inv_e[:])
+        nc.vector.tensor_mul(out=mean, in0=sum_x[:], in1=inv_e[:])
         pooled = back_pool.tile([P, 2 * C], F32, name="back")
         for q in range(HALVES):
             nc.tensor.transpose(
                 out=pooled[:, q * P : (q + 1) * P], in_=v[:, q, :], identity=ident[:]
             )
-        nc.vector.tensor_mul(out=mean_sq[:], in0=mean, in1=mean)
         product(n + 2, True)
+        nc.vector.tensor_mul(out=mean_sq[:], in0=mean, in1=mean)
 
         spread = const.tile([P, HALVES, B], F32)
         nc.vector.tensor_mul(out=spread[:], in0=part_exx[:, 1], in1=inv_e[:])

@@ -39,7 +39,7 @@ GROUPS = B * PARTS
 EXP_LAG = PART_SLOTS
 PRODUCT_LAG = PART_SLOTS + 1
 STEPS = SLOTS + PRODUCT_LAG
-EARLY_FRAMES = (32, 384)
+EARLY_FRAMES = (96, 384)
 GPSIMD_PRODUCTS = (11,)
 GPSIMD_FRAMES = 128
 BRIDGE_SLOT = 5
@@ -47,7 +47,7 @@ BRIDGE_FRAMES = (0, 64)
 BRIDGE_GPSIMD_FRAMES = 384
 WHOLE_FROM = 6
 EXTRA_FROM = 7
-EXTRA_FRAMES = 64
+EXTRA_FRAMES = 112
 HEAD_FRAMES = 320
 
 
@@ -399,8 +399,10 @@ def tile_attentivestatspool_pb_t_kernel(
                 nc.sync.dma_start(out=offset[:], in_=be2.partition_broadcast(B))
             now = units(step)
             now_first = step - PRODUCT_LAG
-            if 0 <= now_first < HALVES * GROUPS:
+            if 0 <= now_first < SLOTS - PRODUCT_LAG:
                 features(now_first)
+            if step == SLOTS - 1:
+                features(SLOTS - PRODUCT_LAG)
             if step < SLOTS:
                 if step > 0:
                     quantise(step)

@@ -39,15 +39,15 @@ GROUPS = B * PARTS
 EXP_LAG = PART_SLOTS
 PRODUCT_LAG = PART_SLOTS + 1
 STEPS = SLOTS + PRODUCT_LAG
-EARLY_FRAMES = (96, 384)
+EARLY_FRAMES = (64, 384)
 GPSIMD_PRODUCTS = (11,)
 GPSIMD_FRAMES = 128
 BRIDGE_SLOT = 5
-BRIDGE_FRAMES = (0, 64)
-BRIDGE_GPSIMD_FRAMES = 384
+BRIDGE_FRAMES = (0, 128)
+BRIDGE_GPSIMD_FRAMES = 256
 WHOLE_FROM = 6
 EXTRA_FROM = 7
-EXTRA_FRAMES = 112
+EXTRA_FRAMES = 32
 HEAD_FRAMES = 320
 
 

@@ -39,15 +39,14 @@ GROUPS = B * PARTS
 EXP_LAG = PART_SLOTS
 PRODUCT_LAG = PART_SLOTS + 1
 STEPS = SLOTS + PRODUCT_LAG
-EARLY_FRAMES = (64, 384)
 GPSIMD_PRODUCTS = (11,)
-GPSIMD_FRAMES = 128
+EARLY_GPSIMD = 64
+EARLY_VECTOR = 416
 BRIDGE_SLOT = 5
-BRIDGE_FRAMES = (0, 128)
-BRIDGE_GPSIMD_FRAMES = 256
+BRIDGE_GPSIMD = 192
+BRIDGE_VECTOR = 0
 WHOLE_FROM = 6
-EXTRA_FROM = 7
-EXTRA_FRAMES = 32
+LATE_GPSIMD = 296
 HEAD_FRAMES = 320
 
 
@@ -56,7 +55,7 @@ def tile_attentivestatspool_pb_t_kernel(
 ):
     nc = tc.nc
     with tc.tile_pool(name="const", bufs=1) as const, tc.tile_pool(
-        name="raw", bufs=8
+        name="raw", bufs=4
     ) as raw_pool, tc.tile_pool(name="grouped", bufs=2) as grouped_pool, tc.tile_pool(
         name="quant", bufs=3
     ) as quant, tc.tile_pool(name="turned", bufs=2) as turned_pool, tc.tile_pool(
@@ -94,10 +93,10 @@ def tile_attentivestatspool_pb_t_kernel(
         def load(s):
             b, c = divmod(s, CHUNKS)
             h_rows = h[b].rearrange("(g p j) n -> g p j n", p=P, j=PACK)
+            raw[s] = raw_pool.tile([P, PASSES, PACK, FRAMES], BF16, name="raw")
             for g in range(PASSES):
-                raw[s, g] = raw_pool.tile([P, PACK, FRAMES], BF16, name="raw")
                 nc.sync.dma_start(
-                    out=raw[s, g][:], in_=h_rows[g, :, :, c * FRAMES : (c + 1) * FRAMES]
+                    out=raw[s][:, g], in_=h_rows[g, :, :, c * FRAMES : (c + 1) * FRAMES]
                 )
 
         def load_x(group):
@@ -112,64 +111,44 @@ def tile_attentivestatspool_pb_t_kernel(
 
         def views(s, g):
             dst = grouped[s][:, g].rearrange("p (c i) j -> p c j i", i=4)
-            src = raw[s, g][:].rearrange("p j (c i) -> p c j i", i=4)
+            src = raw[s][:, g].rearrange("p j (c i) -> p c j i", i=4)
             return dst, src
 
-        def gpsimd_frames(s):
-            if s < 2:
-                return 0
-            if s < WHOLE_FROM:
-                return BRIDGE_GPSIMD_FRAMES if s == BRIDGE_SLOT else GPSIMD_FRAMES
-            return FRAMES
-
-        def vector_frames(s):
+        def shares(s):
             if s >= WHOLE_FROM:
-                return (0, 0)
-            return BRIDGE_FRAMES if s == BRIDGE_SLOT else EARLY_FRAMES
-
-        def gpsimd_copy(s, g, f):
-            nc.gpsimd.tensor_scalar(
-                out=grouped[s][:, g, f:, :],
-                in0=raw[s, g][:, :, f:].rearrange("p j n -> p n j"),
-                scalar1=1.0,
-                scalar2=0.0,
-                op0=ALU.mult,
-                op1=ALU.add,
-            )
+                return LATE_GPSIMD, 0
+            if s == BRIDGE_SLOT:
+                return BRIDGE_GPSIMD, BRIDGE_VECTOR
+            return (EARLY_GPSIMD if s >= 2 else 0), EARLY_VECTOR
 
         def regroup_start(s):
             grouped[s] = grouped_pool.tile(
                 [P, PASSES, FRAMES, PACK], BF16, name="grouped", align_bytes=64
             )
-            if s >= 2:
-                f = FRAMES - gpsimd_frames(s)
-                gpsimd_copy(s, 1, f)
-            if s >= EXTRA_FROM:
-                gpsimd_copy(s, 0, FRAMES - EXTRA_FRAMES)
+            f = FRAMES - shares(s)[0]
+            if f < FRAMES:
+                nc.gpsimd.tensor_scalar(
+                    out=grouped[s][:, :, f:, :],
+                    in0=raw[s][:, :, :, f:].rearrange("p g j n -> p g n j"),
+                    scalar1=1.0,
+                    scalar2=0.0,
+                    op0=ALU.mult,
+                    op1=ALU.add,
+                )
 
-        def regroup_first_pass(s):
-            dst, src = views(s, 0)
-            end = (FRAMES - (EXTRA_FRAMES if s >= EXTRA_FROM else 0)) // 4
-            cut = vector_frames(s)[0] // 4
-            nc.scalar.copy(out=dst[:, cut:end], in_=src[:, cut:end])
-
-        def regroup_second_pass(s):
-            if s >= WHOLE_FROM:
-                return
-            dst, src = views(s, 1)
-            end = (FRAMES - gpsimd_frames(s)) // 4
-            cut = vector_frames(s)[1] // 4
-            if cut < end:
-                nc.scalar.copy(out=dst[:, cut:end], in_=src[:, cut:end])
+        def regroup_scalar(s):
+            gpsimd, vector = shares(s)
+            end = (FRAMES - gpsimd) // 4
+            for g, cut in enumerate((0, vector // 4)):
+                dst, src = views(s, g)
+                if cut < end:
+                    nc.scalar.copy(out=dst[:, cut:end], in_=src[:, cut:end])
 
         def regroup_vector(s):
-            if s >= WHOLE_FROM:
-                return
-            for g in range(PASSES):
-                dst, src = views(s, g)
-                cut = vector_frames(s)[g] // 4
-                if cut > 0:
-                    nc.vector.tensor_copy(out=dst[:, 0:cut], in_=src[:, 0:cut])
+            cut = min(shares(s)[1], FRAMES - shares(s)[0]) // 4
+            dst, src = views(s, 1)
+            if cut > 0:
+                nc.vector.tensor_copy(out=dst[:, 0:cut], in_=src[:, 0:cut])
 
         def quantise(s):
             codes[s] = quant.tile([P, PASSES * FRAMES], U32, name="codes", align_bytes=64)
@@ -436,8 +415,7 @@ def tile_attentivestatspool_pb_t_kernel(
                 else:
                     product(now_first, False)
             if step + 1 < SLOTS:
-                regroup_first_pass(step + 1)
-                regroup_second_pass(step + 1)
+                regroup_scalar(step + 1)
             if step < SLOTS:
                 empty(step)
                 for hf in range(HALVES):

@@ -305,11 +305,9 @@ def tile_attentivestatspool_pb_t_kernel(
                 ex[n] = result
             nc.vector.scalar_tensor_tensor(
                 out=result[:],
-                in0=(ex[n] if second else e[b, part, hf])[:],
+                in0=x_bank[n][:] if in_psum(n) else x_sb[n // HALVES][:, hf, :],
                 scalar=1.0,
-                in1=x_bank[n][:]
-                if in_psum(n)
-                else x_sb[n // HALVES][:, hf, :],
+                in1=(ex[n] if second else e[b, part, hf])[:],
                 op0=ALU.mult,
                 op1=ALU.mult,
                 accum_out=(part_exx if second else part_ex)[:, part, hf, b : b + 1],

@@ -43,7 +43,7 @@ GPSIMD_PRODUCTS = (11,)
 EARLY_GPSIMD = 64
 EARLY_VECTOR = 416
 BRIDGE_SLOT = 5
-BRIDGE_GPSIMD = 192
+BRIDGE_GPSIMD = 160
 BRIDGE_VECTOR = 0
 WHOLE_FROM = 6
 LATE_GPSIMD = 296
@@ -61,7 +61,7 @@ def tile_attentivestatspool_pb_t_kernel(
     ) as quant, tc.tile_pool(name="turned", bufs=2) as turned_pool, tc.tile_pool(
         name="feat", bufs=5
     ) as feat, tc.tile_pool(name="score", bufs=4) as score, tc.tile_pool(
-        name="prod", bufs=2
+        name="prod", bufs=6
     ) as prod, tc.psum_pool(name="acc", bufs=2) as acc_pool, tc.psum_pool(
         name="back", bufs=4
     ) as back_pool, tc.psum_pool(name="xp", bufs=2) as xp_pool, tc.manual_schedule():
@@ -420,8 +420,6 @@ def tile_attentivestatspool_pb_t_kernel(
                     first[step, hf] = turn(step // CHUNKS, step % CHUNKS, hf)
             for b, c, hf in now:
                 exponent(b, c, hf)
-            if now_first in GPSIMD_PRODUCTS:
-                gpsimd_sum(now_first)
 
         n = SLOTS - PRODUCT_LAG
         weight = const.tile([P, HALVES, B], F32)
@@ -433,9 +431,11 @@ def tile_attentivestatspool_pb_t_kernel(
         product(n, False)
         nc.vector.tensor_sub(out=weight[:], in0=neg_max[:, 1], in1=neg_max[:, 0])
         nc.scalar.activation(out=weight[:], in_=weight[:], func=ACT.Exp)
-        nc.scalar.sqrt(out=warm[:], in_=ident[:, 0:1])
         gpsimd_product(n + 1)
+        for early in GPSIMD_PRODUCTS:
+            gpsimd_sum(early)
         gpsimd_sum(n + 1)
+        nc.scalar.sqrt(out=warm[:], in_=ident[:, 0:1])
         product(n, True)
         nc.vector.tensor_reduce(
             out=sum_e2[:],
@@ -447,19 +447,19 @@ def tile_attentivestatspool_pb_t_kernel(
         product(n + 2, False)
         nc.vector.tensor_mul(out=sum_e[:], in0=sum_e2[:, :, :, 0], in1=weight[:])
         nc.vector.tensor_mul(out=base[:], in0=part_exx[:, 0], in1=weight[:])
+        nc.vector.tensor_add(out=sum_x[:], in0=sum_x[:], in1=part_ex[:, 1])
         nc.vector.tensor_add(out=sum_e[:], in0=sum_e[:], in1=sum_e2[:, :, :, 1])
         product(n + 1, True)
         nc.vector.reciprocal(out=inv_e[:], in_=sum_e[:])
-        nc.vector.tensor_add(out=sum_x[:], in0=sum_x[:], in1=part_ex[:, 1])
-        nc.vector.tensor_mul(out=base[:], in0=base[:], in1=inv_e[:])
         nc.vector.tensor_mul(out=mean, in0=sum_x[:], in1=inv_e[:])
+        nc.vector.tensor_mul(out=base[:], in0=base[:], in1=inv_e[:])
         pooled = back_pool.tile([P, 2 * C], F32, name="back")
         for q in range(HALVES):
             nc.tensor.transpose(
                 out=pooled[:, q * P : (q + 1) * P], in_=v[:, q, :], identity=ident[:]
             )
+        nc.scalar.square(out=mean_sq[:], in_=mean)
         product(n + 2, True)
-        nc.vector.tensor_mul(out=mean_sq[:], in0=mean, in1=mean)
 
         spread = const.tile([P, HALVES, B], F32)
         nc.vector.tensor_mul(out=spread[:], in0=part_exx[:, 1], in1=inv_e[:])
@@ -482,22 +482,26 @@ def tile_attentivestatspool_pb_t_kernel(
             out=sd[:], in_=mean_var[:, 1:2], func=ACT.Sqrt, bias=eps_ln[0:B, :], scale=1.0
         )
         result = const.tile([B, 2 * C], F32)
-        nc.vector.scalar_tensor_tensor(
-            out=result[:],
-            in0=pooled[0:B, :],
-            scalar=mean_var[:, 0:1],
-            in1=gain[:],
-            op0=ALU.subtract,
-            op1=ALU.mult,
-        )
         inv_sd = const.tile([B, 1], F32)
-        nc.vector.reciprocal(out=inv_sd[:], in_=sd[:])
-        nc.vector.scalar_tensor_tensor(
-            out=result[:],
-            in0=result[:],
-            scalar=inv_sd[:],
-            in1=offset[:],
-            op0=ALU.mult,
-            op1=ALU.add,
-        )
+        parts = [slice(0, C), slice(C, 2 * C)]
+        for i, cols in enumerate(parts):
+            nc.vector.scalar_tensor_tensor(
+                out=result[:, cols],
+                in0=pooled[0:B, cols],
+                scalar=mean_var[:, 0:1],
+                in1=gain[:, cols],
+                op0=ALU.subtract,
+                op1=ALU.mult,
+            )
+            if i == 0:
+                nc.vector.reciprocal(out=inv_sd[:], in_=sd[:])
+        for cols in parts:
+            nc.vector.scalar_tensor_tensor(
+                out=result[:, cols],
+                in0=result[:, cols],
+                scalar=inv_sd[:],
+                in1=offset[:, cols],
+                op0=ALU.mult,
+                op1=ALU.add,
+            )
         nc.sync.dma_start(out=out.rearrange("b n o -> b (n o)"), in_=result[:])

@@ -41,12 +41,12 @@ PRODUCT_LAG = PART_SLOTS + 1
 STEPS = SLOTS + PRODUCT_LAG
 GPSIMD_PRODUCTS = (11,)
 EARLY_GPSIMD = 64
-EARLY_VECTOR = 416
+EARLY_VECTOR = 448
 BRIDGE_SLOT = 5
 BRIDGE_GPSIMD = 160
 BRIDGE_VECTOR = 0
 WHOLE_FROM = 6
-LATE_GPSIMD = 296
+LATE_GPSIMD = 304
 HEAD_FRAMES = 320
 
 

import concourse.bass as bass
import concourse.mybir as mybir
import concourse.tile as tile
from concourse.masks import make_identity

FLOPS = 2 * 4 * 256 * 1024 * 2048

F32 = mybir.dt.float32
BF16 = mybir.dt.bfloat16
I32 = mybir.dt.int32
U32 = mybir.dt.uint32
U8 = mybir.dt.uint8
FP8X4 = mybir.dt.float8_e4m3fn_x4
FP4X4 = mybir.dt.float4_e2m1fn_x4
ALU = mybir.AluOpType
ACT = mybir.ActivationFunctionType
AX = mybir.AxisListType

P = 128
PACK = 4
K_PASS = P * PACK
B, C, T, H = 4, 256, 2048, 1024
PASSES = H // K_PASS
HALVES = C // P
FRAMES = 512
CHUNKS = T // FRAMES
TILES = FRAMES // P
UTT_TILES = T // P
EPS_LN = 1e-5
EPS_STD = 1e-5
MASKED = 1.0e30

SLOTS = B * CHUNKS
LOAD_AHEAD = 3
PARTS = 2
PART_SLOTS = CHUNKS // PARTS
PART = T // PARTS
GROUPS = B * PARTS
EXP_LAG = PART_SLOTS
PRODUCT_LAG = PART_SLOTS + 1
STEPS = SLOTS + PRODUCT_LAG
GPSIMD_PRODUCTS = (11,)
EARLY_GPSIMD = 64
EARLY_VECTOR = 448
BRIDGE_SLOT = 5
BRIDGE_GPSIMD = 160
BRIDGE_VECTOR = 0
WHOLE_FROM = 6
LATE_GPSIMD = 304
HEAD_FRAMES = 320


def tile_attentivestatspool_pb_t_kernel(
    tc, h, x, mask, w2_words, w2_scales, b2, g2, be2, out
):
    nc = tc.nc
    with tc.tile_pool(name="const", bufs=1) as const, tc.tile_pool(
        name="raw", bufs=4
    ) as raw_pool, tc.tile_pool(name="grouped", bufs=2) as grouped_pool, tc.tile_pool(
        name="quant", bufs=3
    ) as quant, tc.tile_pool(name="turned", bufs=2) as turned_pool, tc.tile_pool(
        name="feat", bufs=5
    ) as feat, tc.tile_pool(name="score", bufs=4) as score, tc.tile_pool(
        name="prod", bufs=6
    ) as prod, tc.psum_pool(name="acc", bufs=2) as acc_pool, tc.psum_pool(
        name="back", bufs=4
    ) as back_pool, tc.psum_pool(name="xp", bufs=2) as xp_pool, tc.manual_schedule():
        ident = const.tile([P, P], F32)
        make_identity(nc, ident[:])
        ident_bf = const.tile([P, P], BF16)
        make_identity(nc, ident_bf[:])
        v = const.tile([P, 2 * HALVES, P], F32)
        nc.gpsimd.memset(v[:], 0.0)
        sum_e4 = const.tile([P, HALVES, B, CHUNKS], F32)
        part_ex = const.tile([P, PARTS, HALVES, B], F32)
        part_exx = const.tile([P, PARTS, HALVES, B], F32)
        neg_max4 = const.tile([P, HALVES, B, CHUNKS], F32)
        neg_max = const.tile([P, PARTS, HALVES, B], F32)

        raw = {}
        grouped = {}
        codes = {}
        planes = {}
        acc = {}
        turned = {}
        first = {}
        again = {}
        x_sb = {}
        x_bank = {}
        e = {}
        ex = {}

        def load(s):
            b, c = divmod(s, CHUNKS)
            h_rows = h[b].rearrange("(g p j) n -> g p j n", p=P, j=PACK)
            raw[s] = raw_pool.tile([P, PASSES, PACK, FRAMES], BF16, name="raw")
            for g in range(PASSES):
                nc.sync.dma_start(
                    out=raw[s][:, g], in_=h_rows[g, :, :, c * FRAMES : (c + 1) * FRAMES]
                )

        def load_x(group):
            b, part = divmod(group, PARTS)
            x_sb[group] = feat.tile([P, HALVES, PART], BF16, name="x_sb")
            nc.sync.dma_start(
                out=x_sb[group][:],
                in_=x[b].rearrange("(hf p) n -> p hf n", p=P)[
                    :, :, part * PART : (part + 1) * PART
                ],
            )

        def views(s, g):
            dst = grouped[s][:, g].rearrange("p (c i) j -> p c j i", i=4)
            src = raw[s][:, g].rearrange("p j (c i) -> p c j i", i=4)
            return dst, src

        def shares(s):
            if s >= WHOLE_FROM:
                return LATE_GPSIMD, 0
            if s == BRIDGE_SLOT:
                return BRIDGE_GPSIMD, BRIDGE_VECTOR
            return (EARLY_GPSIMD if s >= 2 else 0), EARLY_VECTOR

        def regroup_start(s):
            grouped[s] = grouped_pool.tile(
                [P, PASSES, FRAMES, PACK], BF16, name="grouped", align_bytes=64
            )
            f = FRAMES - shares(s)[0]
            if f < FRAMES:
                nc.gpsimd.tensor_scalar(
                    out=grouped[s][:, :, f:, :],
                    in0=raw[s][:, :, :, f:].rearrange("p g j n -> p g n j"),
                    scalar1=1.0,
                    scalar2=0.0,
                    op0=ALU.mult,
                    op1=ALU.add,
                )

        def regroup_scalar(s):
            gpsimd, vector = shares(s)
            end = (FRAMES - gpsimd) // 4
            for g, cut in enumerate((0, vector // 4)):
                dst, src = views(s, g)
                if cut < end:
                    nc.scalar.copy(out=dst[:, cut:end], in_=src[:, cut:end])

        def regroup_vector(s):
            cut = min(shares(s)[1], FRAMES - shares(s)[0]) // 4
            dst, src = views(s, 1)
            if cut > 0:
                nc.vector.tensor_copy(out=dst[:, 0:cut], in_=src[:, 0:cut])

        def quantise(s):
            codes[s] = quant.tile([P, PASSES * FRAMES], U32, name="codes", align_bytes=64)
            planes[s] = quant.tile([P, PASSES * FRAMES], U8, name="planes", align_bytes=64)
            nc.vector.quantize_mx(
                out=codes[s][:].bitcast(FP8X4),
                scales=planes[s][:],
                in_=grouped[s][:].rearrange("p g n j -> p (g n j)"),
            )

        def quantise_pass(s, g):
            if g == 0:
                codes[s] = quant.tile([P, PASSES * FRAMES], U32, name="codes", align_bytes=64)
                planes[s] = quant.tile([P, PASSES * FRAMES], U8, name="planes", align_bytes=64)
            cols = slice(g * FRAMES, (g + 1) * FRAMES)
            nc.vector.quantize_mx(
                out=codes[s][:, cols].bitcast(FP8X4),
                scales=planes[s][:, cols],
                in_=grouped[s][:, g].rearrange("p n j -> p (n j)"),
            )

        def multiply(s):
            for k in range(TILES // 2):
                acc[s, k] = acc_pool.tile([P, 2 * C], F32, name="acc")
            for i in range(TILES):
                for hf in range(HALVES):
                    for g in range(PASSES):
                        cols = slice(g * FRAMES + i * P, g * FRAMES + (i + 1) * P)
                        at = (i % 2) * C + hf * P
                        nc.tensor.matmul_mx(
                            out=acc[s, i // 2][:, at : at + P],
                            lhsT=codes[s][:, cols].bitcast(FP8X4),
                            lhsT_scale=planes[s][:, cols],
                            rhs=w_words[:, g, 2 * P * hf : 2 * P * (hf + 1)].bitcast(FP4X4),
                            rhs_scale=w_planes[:, g, P * hf : P * (hf + 1)],
                            start=(g == 0),
                            stop=(g == PASSES - 1),
                        )

        def empty(s):
            b, c = divmod(s, CHUNKS)
            if c == 0:
                turned[b] = turned_pool.tile([P, UTT_TILES, C], F32, name="turned")
            for i in range(TILES):
                n = c * TILES + i
                nc.scalar.activation(
                    out=turned[b][:, n, :],
                    in_=acc[s, i // 2][:, (i % 2) * C : (i % 2 + 1) * C],
                    func=ACT.Identity,
                    bias=penalty[:, b * UTT_TILES + n : b * UTT_TILES + n + 1],
                    scale=1.0,
                )

        def turn(b, c, hf):
            bank = back_pool.tile([P, FRAMES], F32, name="back")
            for i in range(TILES):
                nc.tensor.transpose(
                    out=bank[:, i * P : (i + 1) * P],
                    in_=turned[b][:, c * TILES + i, hf * P : (hf + 1) * P],
                    identity=ident[:],
                )
            return bank

        def chunk_max(s):
            b, c = divmod(s, CHUNKS)
            for hf in range(HALVES):
                nc.vector.tensor_reduce(
                    out=neg_max4[:, hf, b, c : c + 1],
                    in_=first[s, hf][:],
                    axis=AX.X,
                    op=ALU.max,
                    negate=True,
                )

        def part_max(s):
            b, c = divmod(s, CHUNKS)
            part, last = divmod(c, PART_SLOTS)
            if last == PART_SLOTS - 1:
                nc.vector.tensor_reduce(
                    out=neg_max[:, part, :, b : b + 1],
                    in_=neg_max4[:, :, b, 0 : c + 1],
                    axis=AX.X,
                    op=ALU.min,
                )

        def units(step):
            group, hf = divmod(step - EXP_LAG, HALVES)
            if not 0 <= group < GROUPS:
                return []
            b, part = divmod(group, PARTS)
            return [(b, part * PART_SLOTS + n, hf) for n in range(PART_SLOTS)]

        def exponent(b, c, hf):
            part, n = divmod(c, PART_SLOTS)
            if n == 0:
                e[b, part, hf] = score.tile([P, PART], F32, name="e")
            nc.scalar.activation(
                out=e[b, part, hf][:, n * FRAMES : (n + 1) * FRAMES],
                in_=again[b, c, hf][:],
                func=ACT.Exp,
                bias=neg_max[:, part, hf, b : b + 1],
                scale=1.0,
                accum_out=sum_e4[:, hf, b, c : c + 1],
            )

        def place(n):
            group, hf = divmod(n, HALVES)
            b, part = divmod(group, PARTS)
            return b, part, hf

        def in_psum(n):
            return n < 11 or n == 13

        def features(n):
            if not in_psum(n):
                return
            b, part, hf = place(n)
            bank = xp_pool.tile([P, PART], BF16, name="x_bank")
            x_bank[n] = bank
            for i in range(PART // FRAMES):
                at = i * FRAMES
                nc.tensor.matmul(
                    out=bank[:, i * FRAMES : (i + 1) * FRAMES],
                    lhsT=ident_bf[:],
                    rhs=x_sb[n // HALVES][:, hf, at : at + FRAMES],
                    start=True,
                    stop=True,
                )

        def gpsimd_product(n):
            b, part, hf = place(n)
            ex[n] = prod.tile([P, PART], F32, name="ex")
            nc.gpsimd.tensor_tensor(
                out=ex[n][:],
                in0=e[b, part, hf][:],
                in1=x_sb[n // HALVES][:, hf, :],
                op=ALU.mult,
            )

        def gpsimd_sum(n):
            b, part, hf = place(n)
            spare = score.tile([P, PART], F32, name="spare")
            nc.scalar.activation(
                out=spare[:],
                in_=ex[n][:],
                func=ACT.Copy,
                accum_out=part_ex[:, part, hf, b : b + 1],
            )

        def product(n, second):
            b, part, hf = place(n)
            result = prod.tile([P, PART], F32, name="exx" if second else "ex")
            if not second:
                ex[n] = result
            nc.vector.scalar_tensor_tensor(
                out=result[:],
                in0=x_bank[n][:] if in_psum(n) else x_sb[n // HALVES][:, hf, :],
                scalar=1.0,
                in1=(ex[n] if second else e[b, part, hf])[:],
                op0=ALU.mult,
                op1=ALU.mult,
                accum_out=(part_exx if second else part_ex)[:, part, hf, b : b + 1],
            )

        load(0)
        load(1)
        mask_rows = const.tile([P, P], BF16)
        nc.vector.memset(mask_rows[B * UTT_TILES : P, :], 0.0)
        nc.sync.dma_start(
            out=mask_rows[0 : B * UTT_TILES, :],
            in_=mask.rearrange("b o (i p) -> (b o i) p", p=P),
        )
        w_words = const.tile([P, PASSES, 2 * C], U8, align_bytes=64)
        nc.sync.dma_start(
            out=w_words[:].bitcast(I32),
            in_=w2_words.bitcast(I32).rearrange("g p n -> p g n"),
        )
        w_planes = const.tile([P, PASSES, C], U8, align_bytes=64)
        nc.vector.memset(w_planes[:].rearrange("p g n -> p (g n)").bitcast(I32), 0)
        for q in range(4):
            nc.sync.dma_start(
                out=w_planes[32 * q : 32 * q + 4].bitcast(I32),
                in_=w2_scales.bitcast(I32)[:, 4 * q : 4 * q + 4, :].rearrange(
                    "g r n -> r g n"
                ),
            )
        for s in range(2, LOAD_AHEAD):
            load(s)
        warm = const.tile([P, 1], F32)
        nc.scalar.activation(out=warm[:], in_=ident[:, 0:1], func=ACT.Exp)
        mask_cols = back_pool.tile([P, P], BF16, name="back")
        nc.tensor.transpose(out=mask_cols[:], in_=mask_rows[:], identity=ident_bf[:])
        penalty = const.tile([P, B * UTT_TILES], F32)
        regroup_start(0)
        for g in range(PASSES):
            dst, src = views(0, g)
            nc.vector.tensor_copy(
                out=dst[:, 0 : HEAD_FRAMES // 4], in_=src[:, 0 : HEAD_FRAMES // 4]
            )
            nc.scalar.copy(out=dst[:, HEAD_FRAMES // 4 :], in_=src[:, HEAD_FRAMES // 4 :])
            quantise_pass(0, g)
        regroup_start(1)

        eps_ln = const.tile([P, 1], F32)
        nc.vector.tensor_scalar(
            out=eps_ln[:],
            in0=ident[:, 0:1],
            scalar1=0.0,
            scalar2=EPS_LN,
            op0=ALU.mult,
            op1=ALU.add,
        )
        inv_e = const.tile([P, HALVES, B], F32)
        mean_sq = const.tile([P, HALVES, B], F32)
        gain = const.tile([B, 2 * C], BF16)
        offset = const.tile([B, 2 * C], BF16)
        stats = const.tile([B, 2, 6], F32)
        for step in range(STEPS):
            if step + LOAD_AHEAD < SLOTS:
                load(step + LOAD_AHEAD)
            if step < SLOTS and step % PART_SLOTS == 1:
                load_x(step // PART_SLOTS)
            if step == SLOTS - 1:
                nc.sync.dma_start(out=gain[:], in_=g2.partition_broadcast(B))
                nc.sync.dma_start(out=offset[:], in_=be2.partition_broadcast(B))
            now = units(step)
            now_first = step - PRODUCT_LAG
            if 0 <= now_first < SLOTS - PRODUCT_LAG:
                features(now_first)
            if step == SLOTS - 1:
                features(SLOTS - PRODUCT_LAG)
            if step < SLOTS:
                if step > 0:
                    quantise(step)
                multiply(step)
            for b, c, hf in now:
                again[b, c, hf] = turn(b, c, hf)
            if step + 1 < SLOTS:
                regroup_vector(step + 1)
            if step == 0:
                nc.vector.tensor_scalar(
                    out=penalty[:],
                    in0=mask_cols[:, 0 : B * UTT_TILES],
                    scalar1=MASKED,
                    scalar2=-MASKED,
                    op0=ALU.mult,
                    op1=ALU.add,
                )
            if step + 2 < SLOTS:
                regroup_start(step + 2)
            if 1 <= step <= SLOTS:
                chunk_max(step - 1)
            if step == SLOTS:
                part_max(step - 1)
            if 1 <= now_first <= SLOTS - PRODUCT_LAG:
                product(now_first - 1, True)
            if 1 <= step < SLOTS:
                part_max(step - 1)
            if step < SLOTS and 0 <= now_first:
                if now_first in GPSIMD_PRODUCTS:
                    gpsimd_product(now_first)
                else:
                    product(now_first, False)
            if step + 1 < SLOTS:
                regroup_scalar(step + 1)
            if step < SLOTS:
                empty(step)
                for hf in range(HALVES):
                    first[step, hf] = turn(step // CHUNKS, step % CHUNKS, hf)
            for b, c, hf in now:
                exponent(b, c, hf)

        n = SLOTS - PRODUCT_LAG
        weight = const.tile([P, HALVES, B], F32)
        sum_e2 = const.tile([P, HALVES, B, PARTS], F32)
        sum_e = const.tile([P, HALVES, B], F32)
        sum_x = const.tile([P, HALVES, B], F32)
        base = const.tile([P, HALVES, B], F32)
        mean = v[:, 0:HALVES, 0:B]
        product(n, False)
        nc.vector.tensor_sub(out=weight[:], in0=neg_max[:, 1], in1=neg_max[:, 0])
        nc.scalar.activation(out=weight[:], in_=weight[:], func=ACT.Exp)
        gpsimd_product(n + 1)
        for early in GPSIMD_PRODUCTS:
            gpsimd_sum(early)
        gpsimd_sum(n + 1)
        nc.scalar.sqrt(out=warm[:], in_=ident[:, 0:1])
        product(n, True)
        nc.vector.tensor_reduce(
            out=sum_e2[:],
            in_=sum_e4[:].rearrange("p h b (i c) -> p h b i c", i=PARTS),
            axis=AX.X,
            op=ALU.add,
        )
        nc.vector.tensor_mul(out=sum_x[:], in0=part_ex[:, 0], in1=weight[:])
        product(n + 2, False)
        nc.vector.tensor_mul(out=sum_e[:], in0=sum_e2[:, :, :, 0], in1=weight[:])
        nc.vector.tensor_mul(out=base[:], in0=part_exx[:, 0], in1=weight[:])
        nc.vector.tensor_add(out=sum_x[:], in0=sum_x[:], in1=part_ex[:, 1])
        nc.vector.tensor_add(out=sum_e[:], in0=sum_e[:], in1=sum_e2[:, :, :, 1])
        product(n + 1, True)
        nc.vector.reciprocal(out=inv_e[:], in_=sum_e[:])
        nc.vector.tensor_mul(out=mean, in0=sum_x[:], in1=inv_e[:])
        nc.vector.tensor_mul(out=base[:], in0=base[:], in1=inv_e[:])
        pooled = back_pool.tile([P, 2 * C], F32, name="back")
        for q in range(HALVES):
            nc.tensor.transpose(
                out=pooled[:, q * P : (q + 1) * P], in_=v[:, q, :], identity=ident[:]
            )
        nc.scalar.square(out=mean_sq[:], in_=mean)
        product(n + 2, True)

        spread = const.tile([P, HALVES, B], F32)
        nc.vector.tensor_mul(out=spread[:], in0=part_exx[:, 1], in1=inv_e[:])
        nc.vector.tensor_sub(out=base[:], in0=base[:], in1=mean_sq[:])
        nc.vector.tensor_add(out=spread[:], in0=spread[:], in1=base[:])
        nc.vector.tensor_scalar_max(out=spread[:], in0=spread[:], scalar1=EPS_STD)
        nc.scalar.sqrt(out=v[:, HALVES : 2 * HALVES, 0:B], in_=spread[:])

        nc.vector.bn_stats(out=stats[:, 0, :], in_=pooled[0:B, 0:C])
        for q in range(HALVES, 2 * HALVES):
            nc.tensor.transpose(
                out=pooled[:, q * P : (q + 1) * P], in_=v[:, q, :], identity=ident[:]
            )

        nc.vector.bn_stats(out=stats[:, 1, :], in_=pooled[0:B, C : 2 * C])
        mean_var = const.tile([B, 2], F32)
        nc.vector.bn_aggr(out=mean_var[:], in_=stats[:])
        sd = const.tile([B, 1], F32)
        nc.scalar.activation(
            out=sd[:], in_=mean_var[:, 1:2], func=ACT.Sqrt, bias=eps_ln[0:B, :], scale=1.0
        )
        result = const.tile([B, 2 * C], F32)
        inv_sd = const.tile([B, 1], F32)
        parts = [slice(0, C), slice(C, 2 * C)]
        for i, cols in enumerate(parts):
            nc.vector.scalar_tensor_tensor(
                out=result[:, cols],
                in0=pooled[0:B, cols],
                scalar=mean_var[:, 0:1],
                in1=gain[:, cols],
                op0=ALU.subtract,
                op1=ALU.mult,
            )
            if i == 0:
                nc.vector.reciprocal(out=inv_sd[:], in_=sd[:])
        for cols in parts:
            nc.vector.scalar_tensor_tensor(
                out=result[:, cols],
                in0=result[:, cols],
                scalar=inv_sd[:],
                in1=offset[:, cols],
                op0=ALU.mult,
                op1=ALU.add,
            )
        nc.sync.dma_start(out=out.rearrange("b n o -> b (n o)"), in_=result[:])
